import numpy as np
import ml_dtypes


def mxq(x, axis, fmt="e4m3"):
    dtype, down = {"e4m3": (ml_dtypes.float8_e4m3fn, 7), "e5m2": (ml_dtypes.float8_e5m2, 14)}[fmt]
    v = np.moveaxis(np.asarray(x, np.float32).astype(ml_dtypes.bfloat16).astype(np.float64), axis, -1)
    blocks = v.reshape(v.shape[:-1] + (-1, 32))
    amax = np.abs(blocks).max(-1, keepdims=True)
    byte = np.maximum(np.where(amax > 0, np.frexp(amax)[1] - 1 + 127, 0) - down, 1)
    scale = np.exp2(byte - 127.0)
    codes = (blocks / scale).astype(np.float32).astype(dtype).astype(np.float64)
    return np.moveaxis((codes * scale).reshape(v.shape), -1, axis)


WIDE = False


def mx_kscale(k):
    if not WIDE:
        return np.ones(k)
    levels = np.array([10, -10, 5, -5, 0])
    if k % 512:
        return np.exp2(np.random.permutation(np.resize(levels, k // 32))).repeat(32)
    a = np.empty((k // 512, 16))
    for p in range(k // 512):
        a[p, :8] = np.random.permutation(np.resize(levels, 8))
        for g in range(8):
            far = levels[np.abs(levels - a[p, g]) >= 10]
            a[p, g + 8] = far[np.random.randint(len(far))]
    return np.exp2(a.ravel()).repeat(32)


BF16 = ml_dtypes.bfloat16


def bf(x):
    return np.asarray(x, np.float32).astype(BF16)


def f64(x):
    return np.asarray(x).astype(np.float64)


B, S, D_MODEL, H, NOPE, ROPE = 1, 512, 2048, 4, 256, 128
DK = D_MODEL // H
LAT = 3 * DK
D_HEAD = NOPE + ROPE
D_LATENT = H * D_HEAD
ROT_DIM = 2 * ((ROPE // 2) // 2)
EPS = 1e-6


def rmsnorm(x, w):
    return x * (1.0 / np.sqrt(np.mean(x * x, axis=-1, keepdims=True) + EPS)) * w


def apply_rope(x):
    inv_freq = 1.0 / (10000.0 ** (np.arange(0, ROT_DIM, 2) / ROT_DIM))
    freqs = np.arange(x.shape[-2])[:, None] * inv_freq[None, :]
    freqs = np.repeat(freqs, 2, axis=-1)
    cos, sin = np.cos(freqs), np.sin(freqs)
    xl, xr = x[..., :ROT_DIM], x[..., ROT_DIM:]
    x1, x2 = xl[..., 0::2], xl[..., 1::2]
    rot = np.stack([-x2, x1], axis=-1).reshape(xl.shape)
    return np.concatenate([xl * cos + rot * sin, xr], axis=-1)


def to_heads(t):
    return t.reshape(B, S, D_HEAD, H).transpose(0, 3, 1, 2)


def setup_inputs():
    s, t = mx_kscale(D_MODEL), mx_kscale(LAT)
    return {"x": bf(np.random.standard_normal((B, S, D_MODEL)) * s),
            "w_down": bf(np.random.standard_normal((D_MODEL, LAT)) / np.sqrt(D_MODEL) / s[:, None]),
            "rms_w": bf((1.0 + 0.1 * np.random.standard_normal(LAT)) * t),
            "w_up": bf(np.random.standard_normal((LAT, 3 * D_LATENT)) * 1.25 / np.sqrt(LAT) / t[:, None])}


def reference(x, w_down, rms_w, w_up):
    h = mxq(f64(x), 2, "e4m3") @ mxq(f64(w_down), 0, "e4m3")
    h = rmsnorm(h, f64(rms_w))
    qkv = mxq(h, 2, "e4m3") @ mxq(f64(w_up), 0, "e4m3")
    q, k, v = np.split(qkv, 3, axis=-1)
    q, k, v = to_heads(q), to_heads(k), to_heads(v)
    q_nope, q_rope = q[..., :NOPE], q[..., NOPE:]
    k_nope, k_rope = k[..., :NOPE], k[..., NOPE:]
    q_rope = apply_rope(q_rope)
    k_rope = apply_rope(k_rope)
    return (np.ascontiguousarray(q_nope), q_rope, np.ascontiguousarray(k_nope), k_rope, np.ascontiguousarray(v))

@@ -1,0 +1,469 @@
+from contextlib import ExitStack
+
+import concourse.mybir as mybir
+from concourse.masks import make_identity
+
+F32 = mybir.dt.float32
+BF16 = mybir.dt.bfloat16
+I32 = mybir.dt.int32
+U32 = mybir.dt.uint32
+U8 = mybir.dt.uint8
+FP8X4 = mybir.dt.float8_e4m3fn_x4
+ALU = mybir.AluOpType
+ACT = mybir.ActivationFunctionType
+AXIS = mybir.AxisListType
+
+P = 128
+PACK = 4
+K_PASS = P * PACK
+BANK = 512
+PSUM_BANKS = 8
+
+TOKENS = 512
+TOKEN_TILES = TOKENS // P
+TOKEN_PAIRS = TOKEN_TILES // 2
+D_MODEL = 2048
+LATENT = 1536
+HEADS = 4
+NOPE = 256
+ROPE = 128
+ROTATED = 64
+PAIRS = ROTATED // 2
+D_HEAD = NOPE + ROPE
+THIRD = HEADS * D_HEAD
+THIRDS = 3
+Q, K, V = 0, 1, 2
+TURN = (V, Q, K)
+EPS = 1e-6
+
+DOWN_PASSES = D_MODEL // K_PASS
+UP_PASSES = LATENT // K_PASS
+BLOCKS = LATENT // BANK
+LOADS = DOWN_PASSES + THIRDS * UP_PASSES
+STEPS = LOADS
+RAW_BUFS = 6
+TWO_PI = 6.283185307179586
+ROUND_MAGIC = 12582912.0
+
+FLOPS = 2 * TOKENS * (D_MODEL * LATENT + LATENT * THIRDS * THIRD)
+
+
+def tile_mhlattention_pa_kernel(tc, x, w_down, rms_w, w_up, out_0, out_1, out_2, out_3, out_4):
+    nc = tc.nc
+    with ExitStack() as pools:
+        pools.enter_context(tc.manual_schedule())
+        consts = pools.enter_context(tc.tile_pool(name="consts", bufs=1))
+        raw_pool = pools.enter_context(tc.tile_pool(name="raw", bufs=RAW_BUFS))
+        grouped_pool = pools.enter_context(tc.tile_pool(name="grouped", bufs=2 * BLOCKS))
+        up_pool = pools.enter_context(tc.tile_pool(name="up", bufs=4))
+        keep = pools.enter_context(tc.tile_pool(name="keep", bufs=1))
+        norm_pool = pools.enter_context(tc.tile_pool(name="norm", bufs=2))
+        banks = pools.enter_context(tc.psum_pool(name="banks", bufs=PSUM_BANKS))
+
+        def new_bank(shape, dtype, name):
+            return banks.tile(shape, dtype, name=name, tag="bank")
+
+        ident_f32 = consts.tile([P, P], F32, name="ident_f32")
+        make_identity(nc, ident_f32[:])
+        gain = consts.tile([P, LATENT], BF16, name="gain")
+
+        pos_int = consts.tile([P, TOKEN_TILES], I32, name="pos_int")
+        nc.gpsimd.iota(pos_int[:], pattern=[[1, TOKEN_TILES]], base=0, channel_multiplier=TOKEN_TILES)
+        pos = consts.tile([P, TOKEN_TILES], F32, name="pos")
+        turns = consts.tile([P, 2, PAIRS, TOKEN_TILES], F32, name="turns")
+        whole = consts.tile([P, 2, PAIRS, TOKEN_TILES], F32, name="whole")
+        frac = consts.tile([P, 2, PAIRS, TOKEN_TILES], F32, name="frac")
+        trig = consts.tile([P, 2, PAIRS, TOKEN_TILES], F32, name="trig")
+        cos_rep = consts.tile([P, TOKEN_TILES, PAIRS, 2], F32, name="cos_rep")
+        sin_sign = consts.tile([P, TOKEN_TILES, 2, PAIRS], F32, name="sin_sign")
+        one = consts.tile([P, 1], F32, name="one")
+        one_root = consts.tile([P, 1], F32, name="one_root")
+
+        def angles():
+            nc.vector.tensor_copy(out=pos[:], in_=pos_int[:])
+            nc.vector.tensor_scalar_mul(out=turns[:, 0, 0, :], in0=pos[:], scalar1=1.0 / TWO_PI)
+            done = 1
+            while done < PAIRS:
+                nc.vector.tensor_scalar_mul(
+                    out=turns[:, 0, done : 2 * done, :],
+                    in0=turns[:, 0, 0:done, :],
+                    scalar1=10000.0 ** (-done / PAIRS),
+                )
+                done *= 2
+            nc.vector.tensor_scalar_add(out=turns[:, 1, :, :], in0=turns[:, 0, :, :], scalar1=0.25)
+            nc.vector.tensor_scalar(
+                out=whole[:], in0=turns[:], scalar1=ROUND_MAGIC, scalar2=ROUND_MAGIC, op0=ALU.add, op1=ALU.subtract
+            )
+            nc.vector.tensor_tensor(out=frac[:], in0=turns[:], in1=whole[:], op=ALU.subtract)
+            nc.scalar.activation(out=trig[:], in_=frac[:], func=ACT.Sin, scale=TWO_PI)
+            nc.vector.memset(one[:], 1.0)
+            nc.scalar.activation(out=one_root[:], in_=one[:], func=ACT.Sqrt)
+
+        def rope_tables():
+            nc.vector.tensor_copy(
+                out=cos_rep[:],
+                in_=trig[:, 1, :, :]
+                .rearrange("p i t -> p t i")
+                .unsqueeze(3)
+                .to_broadcast([P, TOKEN_TILES, PAIRS, 2]),
+            )
+            nc.vector.tensor_scalar_mul(
+                out=sin_sign[:, :, 0, :], in0=trig[:, 0, :, :].rearrange("p i t -> p t i"), scalar1=-1.0
+            )
+            nc.vector.tensor_copy(out=sin_sign[:, :, 1, :], in_=trig[:, 0, :, :].rearrange("p i t -> p t i"))
+
+        n_grouped = keep.tile([P, UP_PASSES, TOKEN_TILES, P * PACK], BF16, name="n_grouped", align_bytes=64)
+        n_codes = keep.tile([P, UP_PASSES, TOKEN_TILES, P], U32, name="n_codes", align_bytes=64)
+        n_scales = keep.tile([P, UP_PASSES, TOKEN_TILES, P], U8, name="n_scales", align_bytes=64)
+        sum_sq = keep.tile([P, TOKEN_TILES, BLOCKS], F32, name="sum_sq")
+        sum_copy = keep.tile([P, TOKEN_TILES, BLOCKS], F32, name="sum_copy")
+        total_sq = keep.tile([P, TOKEN_TILES], F32, name="total_sq")
+        rms = keep.tile([P, TOKEN_TILES], F32, name="rms")
+        rstd = keep.tile([P, TOKEN_TILES], F32, name="rstd")
+
+
+        raw_rows = {}
+        step_blocks = {}
+        step_grouped = {}
+        up_codes = {}
+        up_scales = {}
+        asked = [0]
+
+        def fetch_next():
+            load = asked[0]
+            asked[0] += 1
+            if load >= LOADS:
+                return
+            raw = raw_pool.tile([P, PACK, LATENT], BF16, name="raw", tag="raw")
+            raw_rows[load] = raw
+            if load < DOWN_PASSES:
+                pieces = BLOCKS if load == 0 else 1
+                width = LATENT // pieces
+                for piece in range(pieces):
+                    cols = slice(width * piece, width * (piece + 1))
+                    rows = w_down[K_PASS * load : K_PASS * (load + 1), cols]
+                    nc.sync.dma_start(out=raw[:, :, cols], in_=rows.rearrange("(p t) c -> p t c", t=PACK))
+            else:
+                place, g = divmod(load - DOWN_PASSES, UP_PASSES)
+                third = TURN[place]
+                rows = w_up[K_PASS * g : K_PASS * (g + 1), THIRD * third : THIRD * (third + 1)]
+                nc.sync.dma_start(out=raw[:], in_=rows.rearrange("(p t) c -> p t c", t=PACK))
+
+        def blocks_of(s):
+            found = []
+            if s < DOWN_PASSES:
+                for b in range(BLOCKS):
+                    cols = slice(BANK * b, BANK * (b + 1))
+                    found.append((raw_rows[s][:, :, cols], down_codes[:, s, cols], down_scales[:, s, cols]))
+                return found
+            place, part = divmod(s - DOWN_PASSES, BLOCKS)
+            third = TURN[place]
+            for i in range(BLOCKS):
+                g, b = (part, i) if place == 0 else (i, part)
+                if (third, b) not in up_codes:
+                    up_codes[(third, b)] = up_pool.tile(
+                        [P, UP_PASSES, BANK], U32, name="up_codes", tag="up_codes", align_bytes=64
+                    )
+                    up_scales[(third, b)] = up_pool.tile(
+                        [P, UP_PASSES, BANK], U8, name="up_scales", tag="up_scales", align_bytes=64
+                    )
+                raw = raw_rows[DOWN_PASSES + UP_PASSES * place + g]
+                found.append(
+                    (raw[:, :, BANK * b : BANK * (b + 1)], up_codes[(third, b)][:, g, :], up_scales[(third, b)][:, g, :])
+                )
+            return found
+
+        def regroup(s):
+            if s >= STEPS:
+                return
+            step_blocks[s] = blocks_of(s)
+            step_grouped[s] = []
+            for i in range(BLOCKS):
+                grouped = grouped_pool.tile([P, BANK * PACK], BF16, name="grouped", tag="grouped", align_bytes=64)
+                copy = nc.scalar.copy if i == BLOCKS - 1 else nc.vector.tensor_copy
+                copy(
+                    out=grouped[:].rearrange("p (c i t) -> p c t i", i=4, t=PACK),
+                    in_=step_blocks[s][i][0].rearrange("p t (c i) -> p c t i", i=4),
+                )
+                step_grouped[s].append(grouped)
+            if s < DOWN_PASSES + UP_PASSES:
+                fetch_next()
+            elif (s - DOWN_PASSES) % BLOCKS == BLOCKS - 1:
+                for g in range(UP_PASSES):
+                    fetch_next()
+
+        def quantise(s):
+            for i in range(BLOCKS):
+                nc.vector.quantize_mx(
+                    out=step_blocks[s][i][1].bitcast(FP8X4), scales=step_blocks[s][i][2], in_=step_grouped[s][i][:]
+                )
+
+        def step(s):
+            regroup(s + 1)
+            quantise(s)
+
+        x_raw = {}
+
+        def fetch_x(pair):
+            x_raw[pair] = raw_pool.tile([P, 2, D_MODEL], BF16, name="x_raw", tag="raw")
+            nc.sync.dma_start(
+                out=x_raw[pair][:],
+                in_=x[0].rearrange("(p t) k -> p t k", t=TOKEN_TILES)[:, 2 * pair : 2 * pair + 2, :],
+            )
+
+        def quantise_x(pair):
+            for half in range(DOWN_PASSES // 2):
+                x_grouped = grouped_pool.tile([P, BANK * PACK], BF16, name="x_grouped", tag="grouped", align_bytes=64)
+                x_words = x_grouped[:].bitcast(F32).rearrange("q (g t u) -> q g t u", g=2, u=2)
+                for gg in range(2):
+                    g = 2 * half + gg
+                    flipped = new_bank([P, 2, 2 * P], F32, "x_flipped")
+                    for u in range(2):
+                        for tl in range(2):
+                            nc.tensor.transpose(
+                                flipped[:, u, P * tl : P * (tl + 1)],
+                                x_raw[pair][:, tl, :].bitcast(F32)[:, 256 * g + u : 256 * (g + 1) : 2],
+                                ident_f32[:],
+                            )
+                    nc.scalar.copy(out=x_words[:, gg, :, :], in_=flipped[:].rearrange("q u t -> q t u"))
+                passes = slice(2 * half, 2 * half + 2)
+                nc.vector.quantize_mx(
+                    out=x_codes[:, pair, passes, :].rearrange("q g t -> q (g t)").bitcast(FP8X4),
+                    scales=x_scales[:, pair, passes, :].rearrange("q g t -> q (g t)"),
+                    in_=x_grouped[:],
+                )
+
+        h_banks = {}
+
+        def open_h_banks(pair):
+            for t in (2 * pair, 2 * pair + 1):
+                for b in range(BLOCKS):
+                    h_banks[(t, b)] = new_bank([P, BANK], F32, "h_bank")
+
+        def first_pass(t, b, g):
+            pair, tl = divmod(t, 2)
+            tok = slice(P * tl, P * (tl + 1))
+            cols = slice(BANK * b, BANK * (b + 1))
+            nc.tensor.matmul_mx(
+                out=h_banks[(t, b)][:],
+                lhsT=x_codes[:, pair, g, tok].bitcast(FP8X4),
+                lhsT_scale=x_scales[:, pair, g, tok],
+                rhs=down_codes[:, g, cols].bitcast(FP8X4),
+                rhs_scale=down_scales[:, g, cols],
+                start=(g == 0),
+                stop=(g == DOWN_PASSES - 1),
+            )
+
+        def squares(pair):
+            for t in (2 * pair, 2 * pair + 1):
+                for b in range(BLOCKS):
+                    unread = norm_pool.tile([P, BANK], BF16, name="unread", tag="unread", bufs=4)
+                    nc.scalar.activation(
+                        out=unread[:], in_=h_banks[(t, b)][:], func=ACT.Square, accum_out=sum_sq[:, t, b : b + 1]
+                    )
+                nc.scalar.activation(
+                    out=sum_copy[:, t, :], in_=sum_sq[:, t, :], func=ACT.Copy, accum_out=total_sq[:, t : t + 1]
+                )
+            two = slice(2 * pair, 2 * pair + 2)
+            nc.scalar.activation(out=rms[:, two], in_=total_sq[:, two], func=ACT.Sqrt, scale=1.0 / LATENT, bias=EPS)
+
+        n_bf = {}
+
+        def scale(pair):
+            two = slice(2 * pair, 2 * pair + 2)
+            nc.vector.reciprocal(out=rstd[:, two], in_=rms[:, two])
+            for t in (2 * pair, 2 * pair + 1):
+                n_bf[t] = norm_pool.tile([P, LATENT], BF16, name="n_bf", tag="n_bf", bufs=4)
+                for b in range(BLOCKS):
+                    cols = slice(BANK * b, BANK * (b + 1))
+                    nc.vector.scalar_tensor_tensor(
+                        out=n_bf[t][:, cols],
+                        in0=h_banks[(t, b)][:],
+                        scalar=rstd[:, t : t + 1],
+                        in1=gain[:, cols],
+                        op0=ALU.mult,
+                        op1=ALU.mult,
+                    )
+
+        def flip(pair):
+            for g in range(UP_PASSES):
+                flipped = new_bank([P, 2, 2 * P], F32, "n_flipped")
+                for u in range(2):
+                    for tl in range(2):
+                        nc.tensor.transpose(
+                            flipped[:, u, P * tl : P * (tl + 1)],
+                            n_bf[2 * pair + tl][:].bitcast(F32)[:, 256 * g + u : 256 * (g + 1) : 2],
+                            ident_f32[:],
+                        )
+                nc.scalar.copy(
+                    out=n_grouped[:, g, 2 * pair : 2 * pair + 2, :]
+                    .rearrange("p t c -> p (t c)")
+                    .bitcast(F32)
+                    .rearrange("q (r u) -> q r u", u=2),
+                    in_=flipped[:].rearrange("q u r -> q r u"),
+                )
+
+        def quantise_n(pair):
+            two = slice(2 * pair, 2 * pair + 2)
+            for g in range(UP_PASSES):
+                nc.vector.quantize_mx(
+                    out=n_codes[:, g, two, :].rearrange("p t r -> p (t r)").bitcast(FP8X4),
+                    scales=n_scales[:, g, two, :].rearrange("p t r -> p (t r)"),
+                    in_=n_grouped[:, g, two, :].rearrange("p t c -> p (t c)"),
+                )
+
+        outputs = [(out_0, out_1), (out_2, out_3), (out_4, None)]
+        staged = {}
+        split = 2 * HEADS * NOPE
+
+        qkv_banks = {}
+
+        def views(third, pair):
+            whole_tile = staged[(third, pair)]
+            if outputs[third][1] is None:
+                return whole_tile[:].rearrange("p (h t d) -> p h t d", h=HEADS, t=2), None
+            return (
+                whole_tile[:, 0:split].rearrange("p (h t d) -> p h t d", h=HEADS, t=2),
+                whole_tile[:, split:].rearrange("p (h t d) -> p h t d", h=HEADS, t=2),
+            )
+
+        def second(third, b, pairs, copies):
+            tiles = [2 * pair + tl for pair in pairs for tl in range(2)]
+            filled = {}
+            for t in tiles:
+                filled[t] = new_bank([P, BANK], F32, "qkv_bank")
+            for g in range(UP_PASSES):
+                for t in tiles:
+                    nc.tensor.matmul_mx(
+                        out=filled[t][:],
+                        lhsT=n_codes[:, g, t, :].bitcast(FP8X4),
+                        lhsT_scale=n_scales[:, g, t, :],
+                        rhs=up_codes[(third, b)][:, g, :].bitcast(FP8X4),
+                        rhs_scale=up_scales[(third, b)][:, g, :],
+                        start=(g == 0),
+                        stop=(g == UP_PASSES - 1),
+                    )
+            for t in tiles:
+                pair, tl = divmod(t, 2)
+                if b == 0 and tl == 0:
+                    staged[(third, pair)] = stage_pool.tile([P, 2 * THIRD], F32, name="staged", tag="staged")
+                plain, rope = views(third, pair)
+                if rope is not None and P * b >= NOPE:
+                    target = rope[:, :, tl, :]
+                else:
+                    target = plain[:, :, tl, P * b : P * (b + 1)]
+                copies[t % len(copies)](out=target, in_=filled[t][:].rearrange("p (d h) -> p h d", h=HEADS))
+
+        def store_plain(third, pair):
+            tokens = slice(2 * pair, 2 * pair + 2)
+            nc.sync.dma_start(
+                out=outputs[third][0][0].rearrange("h (p t) d -> p h t d", t=TOKEN_TILES)[:, :, tokens, :],
+                in_=views(third, pair)[0],
+            )
+
+        def rotate(third, pair):
+            rope = views(third, pair)[1]
+            rope_out = outputs[third][1]
+            tokens = slice(2 * pair, 2 * pair + 2)
+            rotated = rope[:, :, :, 0:ROTATED]
+            partner = rotated.rearrange("p h t (i e) -> p h t i e", e=2)
+            swapped = swap_pool.tile([P, HEADS, 2, 2, PAIRS], F32, name="swapped", tag="swapped")
+            for e in range(2):
+                nc.vector.tensor_tensor(
+                    out=swapped[:, :, :, e, :],
+                    in0=partner[:, :, :, :, 1 - e],
+                    in1=sin_sign[:, tokens, e, :].unsqueeze(1).to_broadcast([P, HEADS, 2, PAIRS]),
+                    op=ALU.mult,
+                )
+            nc.vector.tensor_tensor(
+                out=rotated,
+                in0=rotated,
+                in1=cos_rep[:, tokens, :, :]
+                .rearrange("p t i e -> p t (i e)")
+                .unsqueeze(1)
+                .to_broadcast([P, HEADS, 2, ROTATED]),
+                op=ALU.mult,
+            )
+            rows = rotated.rearrange("p h t (i e) -> p (h t) i e", e=2)
+            nc.vector.tensor_tensor(
+                out=rows, in0=rows, in1=swapped[:].rearrange("p h t e i -> p (h t) i e"), op=ALU.add
+            )
+            nc.sync.dma_start(
+                out=rope_out[0].rearrange("h (p t) d -> p h t d", t=TOKEN_TILES)[:, :, tokens, :], in_=rope
+            )
+
+        with tc.tile_pool(name="first", bufs=1) as first_pool:
+            down_codes = first_pool.tile([P, DOWN_PASSES, LATENT], U32, name="down_codes", align_bytes=64)
+            down_scales = first_pool.tile([P, DOWN_PASSES, LATENT], U8, name="down_scales", align_bytes=64)
+            x_codes = first_pool.tile([P, TOKEN_PAIRS, DOWN_PASSES, 2 * P], U32, name="x_codes", align_bytes=64)
+            x_scales = first_pool.tile([P, TOKEN_PAIRS, DOWN_PASSES, 2 * P], U8, name="x_scales", align_bytes=64)
+            by_scalar = [nc.scalar.copy]
+            by_both = [nc.scalar.copy, nc.vector.tensor_copy]
+            fetch_next()
+            fetch_next()
+            fetch_x(0)
+            fetch_x(1)
+            fetch_next()
+            fetch_next()
+            regroup(0)
+            angles()
+            step(0)
+            quantise_x(0)
+            fetch_next()
+            rope_tables()
+            quantise_x(1)
+            fetch_next()
+            nc.sync.dma_start(out=gain[:], in_=rms_w.partition_broadcast(P))
+            open_h_banks(0)
+            for t in range(2):
+                for b in range(BLOCKS):
+                    first_pass(t, b, 0)
+            for g in range(1, DOWN_PASSES):
+                step(g)
+                for t in range(2):
+                    for b in range(BLOCKS):
+                        first_pass(t, b, g)
+            squares(0)
+            step(4)
+            regroup(6)
+            scale(0)
+            open_h_banks(1)
+            for t in range(2, TOKEN_TILES):
+                for b in range(BLOCKS):
+                    for g in range(DOWN_PASSES):
+                        first_pass(t, b, g)
+        with tc.tile_pool(name="stage", bufs=4, reuse_waits="tile") as stage_pool, tc.tile_pool(
+            name="swap", bufs=2, reuse_waits="tile"
+        ) as swap_pool:
+            quantise(5)
+            squares(1)
+            flip(0)
+            regroup(7)
+            scale(1)
+            quantise_n(0)
+            flip(1)
+            quantise(6)
+            for b in range(BLOCKS):
+                second(V, b, [0], by_scalar)
+            store_plain(V, 0)
+            step(7)
+            quantise_n(1)
+            for b in range(BLOCKS):
+                second(V, b, [1], by_scalar)
+            store_plain(V, 1)
+            step(8)
+            for s in range(DOWN_PASSES + BLOCKS, STEPS):
+                place, b = divmod(s - DOWN_PASSES, BLOCKS)
+                third = TURN[place]
+                last = s + 1 == STEPS
+                second(third, b, [0, 1], by_both if last else by_scalar)
+                for pair in range(TOKEN_PAIRS):
+                    if b == 1:
+                        store_plain(third, pair)
+                    if last:
+                        rotate(third, pair)
+                if s + 2 < STEPS:
+                    step(s + 2)
+                if b == 2 and not last:
+                    rotate(third, 0)
+                    rotate(third, 1)

@@ -17,7 +17,8 @@ P = 128
 PACK = 4
 K_PASS = P * PACK
 BANK = 512
-PSUM_BANKS = 8
+SUM_BANKS = 6
+MOVE_BANKS = 2
 
 TOKENS = 512
 TOKEN_TILES = TOKENS // P
@@ -34,14 +35,18 @@ THIRD = HEADS * D_HEAD
 THIRDS = 3
 Q, K, V = 0, 1, 2
 TURN = (V, Q, K)
+COLUMN_TURN = (2, 0, 1)
 EPS = 1e-6
+SHARES = ["VVS","VVS","VST","VST","VTT","VTT","VVS","VVS","VVS","VVS","VVS","VVS","VVS"]
 
 DOWN_PASSES = D_MODEL // K_PASS
 UP_PASSES = LATENT // K_PASS
 BLOCKS = LATENT // BANK
 LOADS = DOWN_PASSES + THIRDS * UP_PASSES
 STEPS = LOADS
-RAW_BUFS = 6
+GROUPED_BUFS = 6
+FIRST_FULL_STEP = 9
+RAW_BUFS = 7
 TWO_PI = 6.283185307179586
 ROUND_MAGIC = 12582912.0
 
@@ -51,24 +56,28 @@ FLOPS = 2 * TOKENS * (D_MODEL * LATENT + LATENT * THIRDS * THIRD)
 def tile_mhlattention_pa_kernel(tc, x, w_down, rms_w, w_up, out_0, out_1, out_2, out_3, out_4):
     nc = tc.nc
     with ExitStack() as pools:
-        pools.enter_context(tc.manual_schedule())
         consts = pools.enter_context(tc.tile_pool(name="consts", bufs=1))
         raw_pool = pools.enter_context(tc.tile_pool(name="raw", bufs=RAW_BUFS))
-        grouped_pool = pools.enter_context(tc.tile_pool(name="grouped", bufs=2 * BLOCKS))
+        grouped_pool = pools.enter_context(tc.tile_pool(name="grouped", bufs=GROUPED_BUFS))
         up_pool = pools.enter_context(tc.tile_pool(name="up", bufs=4))
         keep = pools.enter_context(tc.tile_pool(name="keep", bufs=1))
         norm_pool = pools.enter_context(tc.tile_pool(name="norm", bufs=2))
-        banks = pools.enter_context(tc.psum_pool(name="banks", bufs=PSUM_BANKS))
+        psum = pools.enter_context(tc.psum_pool(name="psum", bufs=SUM_BANKS))
 
-        def new_bank(shape, dtype, name):
-            return banks.tile(shape, dtype, name=name, tag="bank")
+        def sum_bank(shape, name):
+            return psum.tile(shape, F32, name=name, tag="sums", bufs=SUM_BANKS)
 
+        def move_bank(shape, dtype, name):
+            return psum.tile(shape, dtype, name=name, tag="moves", bufs=MOVE_BANKS)
+
+        pos_int = consts.tile([P, TOKEN_TILES], I32, name="pos_int")
+        nc.gpsimd.iota(pos_int[:], pattern=[[1, TOKEN_TILES]], base=0, channel_multiplier=TOKEN_TILES)
+        ident_bf = consts.tile([P, P], BF16, name="ident_bf")
+        make_identity(nc, ident_bf[:])
         ident_f32 = consts.tile([P, P], F32, name="ident_f32")
         make_identity(nc, ident_f32[:])
         gain = consts.tile([P, LATENT], BF16, name="gain")
 
-        pos_int = consts.tile([P, TOKEN_TILES], I32, name="pos_int")
-        nc.gpsimd.iota(pos_int[:], pattern=[[1, TOKEN_TILES]], base=0, channel_multiplier=TOKEN_TILES)
         pos = consts.tile([P, TOKEN_TILES], F32, name="pos")
         turns = consts.tile([P, 2, PAIRS, TOKEN_TILES], F32, name="turns")
         whole = consts.tile([P, 2, PAIRS, TOKEN_TILES], F32, name="whole")
@@ -80,23 +89,24 @@ def tile_mhlattention_pa_kernel(tc, x, w_down, rms_w, w_up, out_0, out_1, out_2,
         one_root = consts.tile([P, 1], F32, name="one_root")
 
         def angles():
+            nc.vector.memset(one[:], 1.0)
+            nc.scalar.activation(out=one_root[:], in_=one[:], func=ACT.Sin)
             nc.vector.tensor_copy(out=pos[:], in_=pos_int[:])
             nc.vector.tensor_scalar_mul(out=turns[:, 0, 0, :], in0=pos[:], scalar1=1.0 / TWO_PI)
-            done = 1
-            while done < PAIRS:
+            ready = 1
+            while ready < PAIRS:
                 nc.vector.tensor_scalar_mul(
-                    out=turns[:, 0, done : 2 * done, :],
-                    in0=turns[:, 0, 0:done, :],
-                    scalar1=10000.0 ** (-done / PAIRS),
+                    out=turns[:, 0, ready : 2 * ready, :],
+                    in0=turns[:, 0, 0:ready, :],
+                    scalar1=10000.0 ** (-ready / PAIRS),
                 )
-                done *= 2
+                ready *= 2
             nc.vector.tensor_scalar_add(out=turns[:, 1, :, :], in0=turns[:, 0, :, :], scalar1=0.25)
             nc.vector.tensor_scalar(
                 out=whole[:], in0=turns[:], scalar1=ROUND_MAGIC, scalar2=ROUND_MAGIC, op0=ALU.add, op1=ALU.subtract
             )
             nc.vector.tensor_tensor(out=frac[:], in0=turns[:], in1=whole[:], op=ALU.subtract)
             nc.scalar.activation(out=trig[:], in_=frac[:], func=ACT.Sin, scale=TWO_PI)
-            nc.vector.memset(one[:], 1.0)
             nc.scalar.activation(out=one_root[:], in_=one[:], func=ACT.Sqrt)
 
         def rope_tables():
@@ -123,8 +133,8 @@ def tile_mhlattention_pa_kernel(tc, x, w_down, rms_w, w_up, out_0, out_1, out_2,
 
 
         raw_rows = {}
-        step_blocks = {}
-        step_grouped = {}
+        blocks = {}
+        grouped_blocks = {}
         up_codes = {}
         up_scales = {}
         asked = [0]
@@ -134,78 +144,99 @@ def tile_mhlattention_pa_kernel(tc, x, w_down, rms_w, w_up, out_0, out_1, out_2,
             asked[0] += 1
             if load >= LOADS:
                 return
+            if load == 0:
+                raw = raw_pool.tile([P, BLOCKS, PACK, BANK], BF16, name="raw", tag="raw")
+                for i in range(BLOCKS):
+                    rows = w_down[0:K_PASS, BANK * i : BANK * (i + 1)]
+                    nc.sync.dma_start(out=raw[:, i, :, :], in_=rows.rearrange("(p t) c -> p t c", t=PACK))
+                raw_rows[load] = raw
+                return
             raw = raw_pool.tile([P, PACK, LATENT], BF16, name="raw", tag="raw")
             raw_rows[load] = raw
             if load < DOWN_PASSES:
-                pieces = BLOCKS if load == 0 else 1
-                width = LATENT // pieces
-                for piece in range(pieces):
-                    cols = slice(width * piece, width * (piece + 1))
-                    rows = w_down[K_PASS * load : K_PASS * (load + 1), cols]
-                    nc.sync.dma_start(out=raw[:, :, cols], in_=rows.rearrange("(p t) c -> p t c", t=PACK))
+                rows = w_down[K_PASS * load : K_PASS * (load + 1), :]
+                nc.sync.dma_start(out=raw[:], in_=rows.rearrange("(p t) c -> p t c", t=PACK))
             else:
                 place, g = divmod(load - DOWN_PASSES, UP_PASSES)
                 third = TURN[place]
                 rows = w_up[K_PASS * g : K_PASS * (g + 1), THIRD * third : THIRD * (third + 1)]
                 nc.sync.dma_start(out=raw[:], in_=rows.rearrange("(p t) c -> p t c", t=PACK))
 
-        def blocks_of(s):
-            found = []
+        def block_of(k):
+            s, i = divmod(k, BLOCKS)
             if s < DOWN_PASSES:
-                for b in range(BLOCKS):
-                    cols = slice(BANK * b, BANK * (b + 1))
-                    found.append((raw_rows[s][:, :, cols], down_codes[:, s, cols], down_scales[:, s, cols]))
-                return found
+                cols = slice(BANK * i, BANK * (i + 1))
+                raw = raw_rows[s][:, i, :, :] if s == 0 else raw_rows[s][:, :, cols]
+                return raw, down_codes[:, s, cols], down_scales[:, s, cols]
             place, part = divmod(s - DOWN_PASSES, BLOCKS)
             third = TURN[place]
-            for i in range(BLOCKS):
-                g, b = (part, i) if place == 0 else (i, part)
-                if (third, b) not in up_codes:
-                    up_codes[(third, b)] = up_pool.tile(
-                        [P, UP_PASSES, BANK], U32, name="up_codes", tag="up_codes", align_bytes=64
-                    )
-                    up_scales[(third, b)] = up_pool.tile(
-                        [P, UP_PASSES, BANK], U8, name="up_scales", tag="up_scales", align_bytes=64
-                    )
-                raw = raw_rows[DOWN_PASSES + UP_PASSES * place + g]
-                found.append(
-                    (raw[:, :, BANK * b : BANK * (b + 1)], up_codes[(third, b)][:, g, :], up_scales[(third, b)][:, g, :])
+            g, b = (part, i) if place == 0 else (i, COLUMN_TURN[part])
+            if (third, b) not in up_codes:
+                up_codes[(third, b)] = up_pool.tile(
+                    [P, UP_PASSES, BANK], U32, name="up_codes", tag="up_codes", align_bytes=64
                 )
-            return found
+                up_scales[(third, b)] = up_pool.tile(
+                    [P, UP_PASSES, BANK], U8, name="up_scales", tag="up_scales", align_bytes=64
+                )
+            raw = raw_rows[DOWN_PASSES + UP_PASSES * place + g]
+            return (
+                raw[:, :, BANK * b : BANK * (b + 1)],
+                up_codes[(third, b)][:, g, :],
+                up_scales[(third, b)][:, g, :],
+            )
 
-        def regroup(s):
-            if s >= STEPS:
-                return
-            step_blocks[s] = blocks_of(s)
-            step_grouped[s] = []
-            for i in range(BLOCKS):
-                grouped = grouped_pool.tile([P, BANK * PACK], BF16, name="grouped", tag="grouped", align_bytes=64)
-                copy = nc.scalar.copy if i == BLOCKS - 1 else nc.vector.tensor_copy
+        def lay(k):
+            s, i = divmod(k, BLOCKS)
+            blocks[k] = block_of(k)
+            grouped = grouped_pool.tile([P, BANK * PACK], BF16, name="grouped", tag="grouped", align_bytes=64)
+            grouped_blocks[k] = grouped
+            raw = blocks[k][0]
+            who = SHARES[s][i]
+            if who == "T":
+                for half in range(2):
+                    moved = move_bank([P, 2, BANK], BF16, "moved")
+                    for part in range(2):
+                        first_col = 256 * half + P * part
+                        nc.tensor.matmul(
+                            moved[:, part, :],
+                            lhsT=ident_bf[:],
+                            rhs=raw[:, :, first_col : first_col + P].rearrange("p t c -> p c t"),
+                            start=True,
+                            stop=True,
+                        )
+                    nc.scalar.copy(
+                        out=grouped[:, 2 * BANK * half : 2 * BANK * (half + 1)].bitcast(F32),
+                        in_=moved[:].rearrange("p a c -> p (a c)").bitcast(F32),
+                    )
+            else:
+                copy = nc.scalar.copy if who == "S" else nc.vector.tensor_copy
                 copy(
                     out=grouped[:].rearrange("p (c i t) -> p c t i", i=4, t=PACK),
-                    in_=step_blocks[s][i][0].rearrange("p t (c i) -> p c t i", i=4),
+                    in_=raw.rearrange("p t (c i) -> p c t i", i=4),
                 )
-                step_grouped[s].append(grouped)
-            if s < DOWN_PASSES + UP_PASSES:
+            if i == BLOCKS - 1 and s < DOWN_PASSES + UP_PASSES:
                 fetch_next()
-            elif (s - DOWN_PASSES) % BLOCKS == BLOCKS - 1:
-                for g in range(UP_PASSES):
-                    fetch_next()
 
-        def quantise(s):
-            for i in range(BLOCKS):
-                nc.vector.quantize_mx(
-                    out=step_blocks[s][i][1].bitcast(FP8X4), scales=step_blocks[s][i][2], in_=step_grouped[s][i][:]
-                )
+        def quantise(k):
+            nc.vector.quantize_mx(out=blocks[k][1].bitcast(FP8X4), scales=blocks[k][2], in_=grouped_blocks[k][:])
 
-        def step(s):
-            regroup(s + 1)
-            quantise(s)
+        done = {"laid": 0, "quantised": 0}
+
+        def lay_to(k):
+            while done["laid"] < min(k, STEPS * BLOCKS):
+                lay(done["laid"])
+                done["laid"] += 1
+
+        def prepare(k, lead=0):
+            while done["quantised"] < k:
+                lay_to(done["quantised"] + 1 + lead)
+                quantise(done["quantised"])
+                done["quantised"] += 1
 
         x_raw = {}
 
         def fetch_x(pair):
-            x_raw[pair] = raw_pool.tile([P, 2, D_MODEL], BF16, name="x_raw", tag="raw")
+            x_raw[pair] = first_pool.tile([P, 2, D_MODEL], BF16, name="x_raw", tag="x_raw", bufs=TOKEN_PAIRS)
             nc.sync.dma_start(
                 out=x_raw[pair][:],
                 in_=x[0].rearrange("(p t) k -> p t k", t=TOKEN_TILES)[:, 2 * pair : 2 * pair + 2, :],
@@ -217,7 +248,7 @@ def tile_mhlattention_pa_kernel(tc, x, w_down, rms_w, w_up, out_0, out_1, out_2,
                 x_words = x_grouped[:].bitcast(F32).rearrange("q (g t u) -> q g t u", g=2, u=2)
                 for gg in range(2):
                     g = 2 * half + gg
-                    flipped = new_bank([P, 2, 2 * P], F32, "x_flipped")
+                    flipped = sum_bank([P, 2, 2 * P], "x_flipped")
                     for u in range(2):
                         for tl in range(2):
                             nc.tensor.transpose(
@@ -235,59 +266,57 @@ def tile_mhlattention_pa_kernel(tc, x, w_down, rms_w, w_up, out_0, out_1, out_2,
 
         h_banks = {}
 
-        def open_h_banks(pair):
-            for t in (2 * pair, 2 * pair + 1):
-                for b in range(BLOCKS):
-                    h_banks[(t, b)] = new_bank([P, BANK], F32, "h_bank")
+        def open_h_banks(t):
+            for b in range(BLOCKS):
+                h_banks[(t, b)] = sum_bank([P, BANK], "h_bank")
 
-        def first_pass(t, b, g):
+        def first_pass(t, g):
             pair, tl = divmod(t, 2)
             tok = slice(P * tl, P * (tl + 1))
-            cols = slice(BANK * b, BANK * (b + 1))
-            nc.tensor.matmul_mx(
-                out=h_banks[(t, b)][:],
-                lhsT=x_codes[:, pair, g, tok].bitcast(FP8X4),
-                lhsT_scale=x_scales[:, pair, g, tok],
-                rhs=down_codes[:, g, cols].bitcast(FP8X4),
-                rhs_scale=down_scales[:, g, cols],
-                start=(g == 0),
-                stop=(g == DOWN_PASSES - 1),
-            )
-
-        def squares(pair):
-            for t in (2 * pair, 2 * pair + 1):
-                for b in range(BLOCKS):
-                    unread = norm_pool.tile([P, BANK], BF16, name="unread", tag="unread", bufs=4)
-                    nc.scalar.activation(
-                        out=unread[:], in_=h_banks[(t, b)][:], func=ACT.Square, accum_out=sum_sq[:, t, b : b + 1]
-                    )
-                nc.scalar.activation(
-                    out=sum_copy[:, t, :], in_=sum_sq[:, t, :], func=ACT.Copy, accum_out=total_sq[:, t : t + 1]
+            for b in range(BLOCKS):
+                cols = slice(BANK * b, BANK * (b + 1))
+                nc.tensor.matmul_mx(
+                    out=h_banks[(t, b)][:],
+                    lhsT=x_codes[:, pair, g, tok].bitcast(FP8X4),
+                    lhsT_scale=x_scales[:, pair, g, tok],
+                    rhs=down_codes[:, g, cols].bitcast(FP8X4),
+                    rhs_scale=down_scales[:, g, cols],
+                    start=(g == 0),
+                    stop=(g == DOWN_PASSES - 1),
                 )
-            two = slice(2 * pair, 2 * pair + 2)
-            nc.scalar.activation(out=rms[:, two], in_=total_sq[:, two], func=ACT.Sqrt, scale=1.0 / LATENT, bias=EPS)
+
+        def squares(t):
+            for b in range(BLOCKS):
+                unread = norm_pool.tile([P, BANK], BF16, name="unread", tag="unread", bufs=2)
+                nc.scalar.activation(
+                    out=unread[:], in_=h_banks[(t, b)][:], func=ACT.Square, accum_out=sum_sq[:, t, b : b + 1]
+                )
+            nc.scalar.activation(
+                out=sum_copy[:, t, :], in_=sum_sq[:, t, :], func=ACT.Copy, accum_out=total_sq[:, t : t + 1]
+            )
+            nc.scalar.activation(
+                out=rms[:, t : t + 1], in_=total_sq[:, t : t + 1], func=ACT.Sqrt, scale=1.0 / LATENT, bias=EPS
+            )
 
         n_bf = {}
 
-        def scale(pair):
-            two = slice(2 * pair, 2 * pair + 2)
-            nc.vector.reciprocal(out=rstd[:, two], in_=rms[:, two])
-            for t in (2 * pair, 2 * pair + 1):
-                n_bf[t] = norm_pool.tile([P, LATENT], BF16, name="n_bf", tag="n_bf", bufs=4)
-                for b in range(BLOCKS):
-                    cols = slice(BANK * b, BANK * (b + 1))
-                    nc.vector.scalar_tensor_tensor(
-                        out=n_bf[t][:, cols],
-                        in0=h_banks[(t, b)][:],
-                        scalar=rstd[:, t : t + 1],
-                        in1=gain[:, cols],
-                        op0=ALU.mult,
-                        op1=ALU.mult,
-                    )
+        def scale(t):
+            nc.vector.reciprocal(out=rstd[:, t : t + 1], in_=rms[:, t : t + 1])
+            n_bf[t] = norm_pool.tile([P, LATENT], BF16, name="n_bf", tag="n_bf", bufs=4)
+            for b in range(BLOCKS):
+                cols = slice(BANK * b, BANK * (b + 1))
+                nc.vector.scalar_tensor_tensor(
+                    out=n_bf[t][:, cols],
+                    in0=h_banks[(t, b)][:],
+                    scalar=rstd[:, t : t + 1],
+                    in1=gain[:, cols],
+                    op0=ALU.mult,
+                    op1=ALU.mult,
+                )
 
         def flip(pair):
             for g in range(UP_PASSES):
-                flipped = new_bank([P, 2, 2 * P], F32, "n_flipped")
+                flipped = move_bank([P, 2, 2 * P], F32, "n_flipped")
                 for u in range(2):
                     for tl in range(2):
                         nc.tensor.transpose(
@@ -331,7 +360,7 @@ def tile_mhlattention_pa_kernel(tc, x, w_down, rms_w, w_up, out_0, out_1, out_2,
             tiles = [2 * pair + tl for pair in pairs for tl in range(2)]
             filled = {}
             for t in tiles:
-                filled[t] = new_bank([P, BANK], F32, "qkv_bank")
+                filled[t] = sum_bank([P, BANK], "qkv_bank")
             for g in range(UP_PASSES):
                 for t in tiles:
                     nc.tensor.matmul_mx(
@@ -345,7 +374,7 @@ def tile_mhlattention_pa_kernel(tc, x, w_down, rms_w, w_up, out_0, out_1, out_2,
                     )
             for t in tiles:
                 pair, tl = divmod(t, 2)
-                if b == 0 and tl == 0:
+                if (third, pair) not in staged:
                     staged[(third, pair)] = stage_pool.tile([P, 2 * THIRD], F32, name="staged", tag="staged")
                 plain, rope = views(third, pair)
                 if rope is not None and P * b >= NOPE:
@@ -359,6 +388,14 @@ def tile_mhlattention_pa_kernel(tc, x, w_down, rms_w, w_up, out_0, out_1, out_2,
             nc.sync.dma_start(
                 out=outputs[third][0][0].rearrange("h (p t) d -> p h t d", t=TOKEN_TILES)[:, :, tokens, :],
                 in_=views(third, pair)[0],
+            )
+
+        def store_block(third, t, b):
+            pair, tl = divmod(t, 2)
+            channels = slice(P * b, P * (b + 1))
+            nc.sync.dma_start(
+                out=outputs[third][0][0].rearrange("h (p t) d -> p h t d", t=TOKEN_TILES)[:, :, t, channels],
+                in_=views(third, pair)[0][:, :, tl, channels],
             )
 
         def rotate(third, pair):
@@ -399,71 +436,90 @@ def tile_mhlattention_pa_kernel(tc, x, w_down, rms_w, w_up, out_0, out_1, out_2,
             x_scales = first_pool.tile([P, TOKEN_PAIRS, DOWN_PASSES, 2 * P], U8, name="x_scales", align_bytes=64)
             by_scalar = [nc.scalar.copy]
             by_both = [nc.scalar.copy, nc.vector.tensor_copy]
-            fetch_next()
-            fetch_next()
+            for load in range(2):
+                fetch_next()
             fetch_x(0)
             fetch_x(1)
-            fetch_next()
-            fetch_next()
-            regroup(0)
-            angles()
-            step(0)
-            quantise_x(0)
-            fetch_next()
-            rope_tables()
-            quantise_x(1)
-            fetch_next()
+            for load in range(2, DOWN_PASSES):
+                fetch_next()
             nc.sync.dma_start(out=gain[:], in_=rms_w.partition_broadcast(P))
-            open_h_banks(0)
+            for load in range(DOWN_PASSES, RAW_BUFS):
+                fetch_next()
+            angles()
+            rope_tables()
+            for g in range(2):
+                lay_to(BLOCKS * (g + 1))
+                prepare(BLOCKS * (g + 1))
+            quantise_x(0)
+            quantise_x(1)
             for t in range(2):
-                for b in range(BLOCKS):
-                    first_pass(t, b, 0)
-            for g in range(1, DOWN_PASSES):
-                step(g)
-                for t in range(2):
-                    for b in range(BLOCKS):
-                        first_pass(t, b, g)
+                open_h_banks(t)
+                for g in range(2):
+                    first_pass(t, g)
+            lay_to(9)
+            prepare(9)
+            for t in range(2):
+                first_pass(t, 2)
+            lay_to(12)
+            prepare(12)
+            for t in range(2):
+                first_pass(t, 3)
+            lay_to(15)
             squares(0)
-            step(4)
-            regroup(6)
+            squares(1)
+            prepare(15)
             scale(0)
-            open_h_banks(1)
-            for t in range(2, TOKEN_TILES):
-                for b in range(BLOCKS):
-                    for g in range(DOWN_PASSES):
-                        first_pass(t, b, g)
+            lay_to(18)
+            scale(1)
+            open_h_banks(2)
+            for g in range(2):
+                first_pass(2, g)
+            flip(0)
+            for g in range(2, 4):
+                first_pass(2, g)
+            squares(2)
+            prepare(18)
+            lay_to(21)
+            quantise_n(0)
+            open_h_banks(3)
+            for g in range(DOWN_PASSES):
+                first_pass(3, g)
+            scale(2)
+            squares(3)
+            prepare(21)
         with tc.tile_pool(name="stage", bufs=4, reuse_waits="tile") as stage_pool, tc.tile_pool(
             name="swap", bufs=2, reuse_waits="tile"
         ) as swap_pool:
-            quantise(5)
-            squares(1)
-            flip(0)
-            regroup(7)
-            scale(1)
-            quantise_n(0)
+            lay_to(24)
+            scale(3)
+            second(V, 0, [0], by_scalar)
             flip(1)
-            quantise(6)
-            for b in range(BLOCKS):
-                second(V, b, [0], by_scalar)
-            store_plain(V, 0)
-            step(7)
+            prepare(23)
             quantise_n(1)
-            for b in range(BLOCKS):
-                second(V, b, [1], by_scalar)
+            prepare(24)
+            lay_to(27)
+            second(V, 1, [0], by_scalar)
+            second(V, 2, [0], by_scalar)
+            store_plain(V, 0)
+            prepare(26, 2)
+            second(V, 0, [1], by_scalar)
+            prepare(27, 2)
+            second(V, 1, [1], by_scalar)
+            second(V, 2, [1], by_scalar)
             store_plain(V, 1)
-            step(8)
+            prepare(28, 2)
             for s in range(DOWN_PASSES + BLOCKS, STEPS):
-                place, b = divmod(s - DOWN_PASSES, BLOCKS)
+                place, part = divmod(s - DOWN_PASSES, BLOCKS)
                 third = TURN[place]
-                last = s + 1 == STEPS
-                second(third, b, [0, 1], by_both if last else by_scalar)
-                for pair in range(TOKEN_PAIRS):
-                    if b == 1:
+                b = COLUMN_TURN[part]
+                second(third, b, [0, 1], by_both if s + 1 == STEPS else by_scalar)
+                if place == 1 and part == 2:
+                    for pair in range(TOKEN_PAIRS):
                         store_plain(third, pair)
-                    if last:
-                        rotate(third, pair)
-                if s + 2 < STEPS:
-                    step(s + 2)
-                if b == 2 and not last:
+                elif place == 2 and part > 0:
+                    for t in range(TOKEN_TILES):
+                        store_block(third, t, b)
+                prepare(min(BLOCKS * (s + 3), BLOCKS * STEPS), 2)
+                if part == 1:
                     rotate(third, 0)
                     rotate(third, 1)

@@ -37,7 +37,7 @@ Q, K, V = 0, 1, 2
 TURN = (V, Q, K)
 COLUMN_TURN = (2, 0, 1)
 EPS = 1e-6
-SHARES = ["VVS","VVS","VST","VST","VTT","VTT","VVS","VVS","VVS","VVS","VVS","VVS","VVS"]
+SHARES = ["VVS","VVS","VVS","VVS","VVS","VVS","VVS","VVS","VVS","VVS","VVS","VVS","VVS"]
 
 DOWN_PASSES = D_MODEL // K_PASS
 UP_PASSES = LATENT // K_PASS

@@ -37,16 +37,15 @@ Q, K, V = 0, 1, 2
 TURN = (V, Q, K)
 COLUMN_TURN = (2, 0, 1)
 EPS = 1e-6
-SHARES = ["VVS","VVS","VVS","VVS","VVS","VVS","VVS","VVS","VVS","VVS","VVS","VVS","VVS"]
+HEAD_PAIRS = (slice(0, 2), slice(2, 4))
 
 DOWN_PASSES = D_MODEL // K_PASS
 UP_PASSES = LATENT // K_PASS
 BLOCKS = LATENT // BANK
 LOADS = DOWN_PASSES + THIRDS * UP_PASSES
 STEPS = LOADS
-GROUPED_BUFS = 6
-FIRST_FULL_STEP = 9
-RAW_BUFS = 7
+GROUPED_BUFS = 3
+RAW_BUFS = 6
 TWO_PI = 6.283185307179586
 ROUND_MAGIC = 12582912.0
 
@@ -59,7 +58,7 @@ def tile_mhlattention_pa_kernel(tc, x, w_down, rms_w, w_up, out_0, out_1, out_2,
         consts = pools.enter_context(tc.tile_pool(name="consts", bufs=1))
         raw_pool = pools.enter_context(tc.tile_pool(name="raw", bufs=RAW_BUFS))
         grouped_pool = pools.enter_context(tc.tile_pool(name="grouped", bufs=GROUPED_BUFS))
-        up_pool = pools.enter_context(tc.tile_pool(name="up", bufs=4))
+        up_pool = pools.enter_context(tc.tile_pool(name="up", bufs=5))
         keep = pools.enter_context(tc.tile_pool(name="keep", bufs=1))
         norm_pool = pools.enter_context(tc.tile_pool(name="norm", bufs=2))
         psum = pools.enter_context(tc.psum_pool(name="psum", bufs=SUM_BANKS))
@@ -72,8 +71,6 @@ def tile_mhlattention_pa_kernel(tc, x, w_down, rms_w, w_up, out_0, out_1, out_2,
 
         pos_int = consts.tile([P, TOKEN_TILES], I32, name="pos_int")
         nc.gpsimd.iota(pos_int[:], pattern=[[1, TOKEN_TILES]], base=0, channel_multiplier=TOKEN_TILES)
-        ident_bf = consts.tile([P, P], BF16, name="ident_bf")
-        make_identity(nc, ident_bf[:])
         ident_f32 = consts.tile([P, P], F32, name="ident_f32")
         make_identity(nc, ident_f32[:])
         gain = consts.tile([P, LATENT], BF16, name="gain")
@@ -133,8 +130,8 @@ def tile_mhlattention_pa_kernel(tc, x, w_down, rms_w, w_up, out_0, out_1, out_2,
 
 
         raw_rows = {}
-        blocks = {}
-        grouped_blocks = {}
+        step_blocks = {}
+        step_grouped = {}
         up_codes = {}
         up_scales = {}
         asked = [0]
@@ -167,70 +164,80 @@ def tile_mhlattention_pa_kernel(tc, x, w_down, rms_w, w_up, out_0, out_1, out_2,
             if s < DOWN_PASSES:
                 cols = slice(BANK * i, BANK * (i + 1))
                 raw = raw_rows[s][:, i, :, :] if s == 0 else raw_rows[s][:, :, cols]
+                raw = raw.rearrange("p t (c i) -> p t c i", i=4)
                 return raw, down_codes[:, s, cols], down_scales[:, s, cols]
             place, part = divmod(s - DOWN_PASSES, BLOCKS)
             third = TURN[place]
             g, b = (part, i) if place == 0 else (i, COLUMN_TURN[part])
             if (third, b) not in up_codes:
                 up_codes[(third, b)] = up_pool.tile(
-                    [P, UP_PASSES, BANK], U32, name="up_codes", tag="up_codes", align_bytes=64
+                    [P, UP_PASSES * BANK], U32, name="up_codes", tag="up_codes", align_bytes=64
                 )
                 up_scales[(third, b)] = up_pool.tile(
-                    [P, UP_PASSES, BANK], U8, name="up_scales", tag="up_scales", align_bytes=64
+                    [P, UP_PASSES * BANK], U8, name="up_scales", tag="up_scales", align_bytes=64
                 )
             raw = raw_rows[DOWN_PASSES + UP_PASSES * place + g]
-            return (
-                raw[:, :, BANK * b : BANK * (b + 1)],
-                up_codes[(third, b)][:, g, :],
-                up_scales[(third, b)][:, g, :],
+            if third != V and b < 2:
+                raw = raw[:, :, 0 : HEADS * NOPE].rearrange("p t (d h) -> p t d h", h=HEADS)[:, :, :, HEAD_PAIRS[b]]
+            else:
+                raw = raw[:, :, BANK * b : BANK * (b + 1)].rearrange("p t (d h) -> p t d h", h=HEADS)
+            words = slice(BANK * g, BANK * (g + 1))
+            return raw, up_codes[(third, b)][:, words], up_scales[(third, b)][:, words]
+
+        def lay_out(copy, raw, grouped):
+            copy(
+                out=grouped.rearrange("p (c i t) -> p c t i", i=raw.shape[3], t=PACK),
+                in_=raw.rearrange("p t c i -> p c t i"),
             )
 
-        def lay(k):
-            s, i = divmod(k, BLOCKS)
-            blocks[k] = block_of(k)
-            grouped = grouped_pool.tile([P, BANK * PACK], BF16, name="grouped", tag="grouped", align_bytes=64)
-            grouped_blocks[k] = grouped
-            raw = blocks[k][0]
-            who = SHARES[s][i]
-            if who == "T":
-                for half in range(2):
-                    moved = move_bank([P, 2, BANK], BF16, "moved")
-                    for part in range(2):
-                        first_col = 256 * half + P * part
-                        nc.tensor.matmul(
-                            moved[:, part, :],
-                            lhsT=ident_bf[:],
-                            rhs=raw[:, :, first_col : first_col + P].rearrange("p t c -> p c t"),
-                            start=True,
-                            stop=True,
-                        )
-                    nc.scalar.copy(
-                        out=grouped[:, 2 * BANK * half : 2 * BANK * (half + 1)].bitcast(F32),
-                        in_=moved[:].rearrange("p a c -> p (a c)").bitcast(F32),
-                    )
+        def lay(s):
+            step_blocks[s] = [block_of(BLOCKS * s + i) for i in range(BLOCKS)]
+            two = grouped_pool.tile([P, 2 * BANK * PACK], BF16, name="two", tag="two", bufs=2, align_bytes=64)
+            one = grouped_pool.tile([P, BANK * PACK], BF16, name="grouped", tag="grouped", align_bytes=64)
+            if 0 < s < DOWN_PASSES + UP_PASSES:
+                both = raw_rows[s][:, :, 0 : 2 * BANK].rearrange("p t (c i) -> p t c i", i=4)
+                lay_out(nc.vector.tensor_copy, both, two[:])
             else:
-                copy = nc.scalar.copy if who == "S" else nc.vector.tensor_copy
-                copy(
-                    out=grouped[:].rearrange("p (c i t) -> p c t i", i=4, t=PACK),
-                    in_=raw.rearrange("p t (c i) -> p c t i", i=4),
-                )
-            if i == BLOCKS - 1 and s < DOWN_PASSES + UP_PASSES:
+                for i in range(2):
+                    lay_out(
+                        nc.vector.tensor_copy, step_blocks[s][i][0], two[:, BANK * PACK * i : BANK * PACK * (i + 1)]
+                    )
+            lay_out(nc.scalar.copy, step_blocks[s][2][0], one[:])
+            step_grouped[s] = (two, one)
+            if s < DOWN_PASSES + UP_PASSES:
                 fetch_next()
 
-        def quantise(k):
-            nc.vector.quantize_mx(out=blocks[k][1].bitcast(FP8X4), scales=blocks[k][2], in_=grouped_blocks[k][:])
+        def quantise_two(s):
+            two = step_grouped[s][0]
+            if s < DOWN_PASSES:
+                quantize(two[:], down_codes[:, s, 0 : 2 * BANK], down_scales[:, s, 0 : 2 * BANK])
+            elif s < DOWN_PASSES + UP_PASSES:
+                for i in range(2):
+                    quantize(two[:, BANK * PACK * i : BANK * PACK * (i + 1)], step_blocks[s][i][1], step_blocks[s][i][2])
+            else:
+                place, part = divmod(s - DOWN_PASSES, BLOCKS)
+                block = (TURN[place], COLUMN_TURN[part])
+                quantize(two[:], up_codes[block][:, 0 : 2 * BANK], up_scales[block][:, 0 : 2 * BANK])
+
+        def quantise_one(s):
+            quantize(step_grouped[s][1][:], step_blocks[s][2][1], step_blocks[s][2][2])
+
+        def quantize(grouped, codes, scales):
+            nc.vector.quantize_mx(out=codes.bitcast(FP8X4), scales=scales, in_=grouped)
 
         done = {"laid": 0, "quantised": 0}
 
-        def lay_to(k):
-            while done["laid"] < min(k, STEPS * BLOCKS):
+        def lay_to(s):
+            while done["laid"] < min(s, STEPS):
                 lay(done["laid"])
                 done["laid"] += 1
 
-        def prepare(k, lead=0):
-            while done["quantised"] < k:
+        def prepare(s, lead):
+            while done["quantised"] < min(s, STEPS):
+                lay_to(done["quantised"] + 1)
+                quantise_two(done["quantised"])
                 lay_to(done["quantised"] + 1 + lead)
-                quantise(done["quantised"])
+                quantise_one(done["quantised"])
                 done["quantised"] += 1
 
         x_raw = {}
@@ -367,8 +374,8 @@ def tile_mhlattention_pa_kernel(tc, x, w_down, rms_w, w_up, out_0, out_1, out_2,
                         out=filled[t][:],
                         lhsT=n_codes[:, g, t, :].bitcast(FP8X4),
                         lhsT_scale=n_scales[:, g, t, :],
-                        rhs=up_codes[(third, b)][:, g, :].bitcast(FP8X4),
-                        rhs_scale=up_scales[(third, b)][:, g, :],
+                        rhs=up_codes[(third, b)][:, BANK * g : BANK * (g + 1)].bitcast(FP8X4),
+                        rhs_scale=up_scales[(third, b)][:, BANK * g : BANK * (g + 1)],
                         start=(g == 0),
                         stop=(g == UP_PASSES - 1),
                     )
@@ -377,25 +384,20 @@ def tile_mhlattention_pa_kernel(tc, x, w_down, rms_w, w_up, out_0, out_1, out_2,
                 if (third, pair) not in staged:
                     staged[(third, pair)] = stage_pool.tile([P, 2 * THIRD], F32, name="staged", tag="staged")
                 plain, rope = views(third, pair)
-                if rope is not None and P * b >= NOPE:
+                if third == V:
+                    target = plain[:, :, tl, P * b : P * (b + 1)]
+                elif b == 2:
                     target = rope[:, :, tl, :]
                 else:
-                    target = plain[:, :, tl, P * b : P * (b + 1)]
-                copies[t % len(copies)](out=target, in_=filled[t][:].rearrange("p (d h) -> p h d", h=HEADS))
+                    target = plain[:, HEAD_PAIRS[b], tl, :]
+                heads = target.shape[1]
+                copies[t % len(copies)](out=target, in_=filled[t][:].rearrange("p (d h) -> p h d", h=heads))
 
-        def store_plain(third, pair):
+        def store_plain(third, pair, heads):
             tokens = slice(2 * pair, 2 * pair + 2)
             nc.sync.dma_start(
-                out=outputs[third][0][0].rearrange("h (p t) d -> p h t d", t=TOKEN_TILES)[:, :, tokens, :],
-                in_=views(third, pair)[0],
-            )
-
-        def store_block(third, t, b):
-            pair, tl = divmod(t, 2)
-            channels = slice(P * b, P * (b + 1))
-            nc.sync.dma_start(
-                out=outputs[third][0][0].rearrange("h (p t) d -> p h t d", t=TOKEN_TILES)[:, :, t, channels],
-                in_=views(third, pair)[0][:, :, tl, channels],
+                out=outputs[third][0][0].rearrange("h (p t) d -> p h t d", t=TOKEN_TILES)[:, heads, tokens, :],
+                in_=views(third, pair)[0][:, heads, :, :],
             )
 
         def rotate(third, pair):
@@ -447,29 +449,22 @@ def tile_mhlattention_pa_kernel(tc, x, w_down, rms_w, w_up, out_0, out_1, out_2,
                 fetch_next()
             angles()
             rope_tables()
-            for g in range(2):
-                lay_to(BLOCKS * (g + 1))
-                prepare(BLOCKS * (g + 1))
+            prepare(2, 0)
             quantise_x(0)
             quantise_x(1)
             for t in range(2):
                 open_h_banks(t)
                 for g in range(2):
                     first_pass(t, g)
-            lay_to(9)
-            prepare(9)
-            for t in range(2):
-                first_pass(t, 2)
-            lay_to(12)
-            prepare(12)
-            for t in range(2):
-                first_pass(t, 3)
-            lay_to(15)
+            for g in range(2, DOWN_PASSES):
+                prepare(g + 1, 0)
+                for t in range(2):
+                    first_pass(t, g)
+            lay_to(5)
             squares(0)
             squares(1)
-            prepare(15)
+            prepare(5, 1)
             scale(0)
-            lay_to(18)
             scale(1)
             open_h_banks(2)
             for g in range(2):
@@ -478,48 +473,38 @@ def tile_mhlattention_pa_kernel(tc, x, w_down, rms_w, w_up, out_0, out_1, out_2,
             for g in range(2, 4):
                 first_pass(2, g)
             squares(2)
-            prepare(18)
-            lay_to(21)
+            prepare(6, 1)
             quantise_n(0)
             open_h_banks(3)
             for g in range(DOWN_PASSES):
                 first_pass(3, g)
             scale(2)
             squares(3)
-            prepare(21)
+            prepare(7, 1)
         with tc.tile_pool(name="stage", bufs=4, reuse_waits="tile") as stage_pool, tc.tile_pool(
             name="swap", bufs=2, reuse_waits="tile"
         ) as swap_pool:
-            lay_to(24)
             scale(3)
             second(V, 0, [0], by_scalar)
             flip(1)
-            prepare(23)
             quantise_n(1)
-            prepare(24)
-            lay_to(27)
+            prepare(8, 1)
             second(V, 1, [0], by_scalar)
             second(V, 2, [0], by_scalar)
-            store_plain(V, 0)
-            prepare(26, 2)
-            second(V, 0, [1], by_scalar)
-            prepare(27, 2)
-            second(V, 1, [1], by_scalar)
-            second(V, 2, [1], by_scalar)
-            store_plain(V, 1)
-            prepare(28, 2)
+            store_plain(V, 0, slice(0, HEADS))
+            for b in range(BLOCKS):
+                second(V, b, [1], by_scalar)
+            store_plain(V, 1, slice(0, HEADS))
+            prepare(9, 1)
             for s in range(DOWN_PASSES + BLOCKS, STEPS):
                 place, part = divmod(s - DOWN_PASSES, BLOCKS)
                 third = TURN[place]
                 b = COLUMN_TURN[part]
                 second(third, b, [0, 1], by_both if s + 1 == STEPS else by_scalar)
-                if place == 1 and part == 2:
+                if b < 2:
                     for pair in range(TOKEN_PAIRS):
-                        store_plain(third, pair)
-                elif place == 2 and part > 0:
-                    for t in range(TOKEN_TILES):
-                        store_block(third, t, b)
-                prepare(min(BLOCKS * (s + 3), BLOCKS * STEPS), 2)
+                        store_plain(third, pair, HEAD_PAIRS[b])
+                prepare(s + 3, 1)
                 if part == 1:
                     rotate(third, 0)
                     rotate(third, 1)

@@ -37,6 +37,7 @@ Q, K, V = 0, 1, 2
 TURN = (V, Q, K)
 COLUMN_TURN = (2, 0, 1)
 EPS = 1e-6
+EXTRA = (5,)
 HEAD_PAIRS = (slice(0, 2), slice(2, 4))
 
 DOWN_PASSES = D_MODEL // K_PASS
@@ -81,7 +82,7 @@ def tile_mhlattention_pa_kernel(tc, x, w_down, rms_w, w_up, out_0, out_1, out_2,
         frac = consts.tile([P, 2, PAIRS, TOKEN_TILES], F32, name="frac")
         trig = consts.tile([P, 2, PAIRS, TOKEN_TILES], F32, name="trig")
         cos_rep = consts.tile([P, TOKEN_TILES, PAIRS, 2], F32, name="cos_rep")
-        sin_sign = consts.tile([P, TOKEN_TILES, 2, PAIRS], F32, name="sin_sign")
+        sin_sign = consts.tile([P, TOKEN_TILES, PAIRS, 2], F32, name="sin_sign")
         one = consts.tile([P, 1], F32, name="one")
         one_root = consts.tile([P, 1], F32, name="one_root")
 
@@ -115,9 +116,9 @@ def tile_mhlattention_pa_kernel(tc, x, w_down, rms_w, w_up, out_0, out_1, out_2,
                 .to_broadcast([P, TOKEN_TILES, PAIRS, 2]),
             )
             nc.vector.tensor_scalar_mul(
-                out=sin_sign[:, :, 0, :], in0=trig[:, 0, :, :].rearrange("p i t -> p t i"), scalar1=-1.0
+                out=sin_sign[:, :, :, 0], in0=trig[:, 0, :, :].rearrange("p i t -> p t i"), scalar1=-1.0
             )
-            nc.vector.tensor_copy(out=sin_sign[:, :, 1, :], in_=trig[:, 0, :, :].rearrange("p i t -> p t i"))
+            nc.vector.tensor_copy(out=sin_sign[:, :, :, 1], in_=trig[:, 0, :, :].rearrange("p i t -> p t i"))
 
         n_grouped = keep.tile([P, UP_PASSES, TOKEN_TILES, P * PACK], BF16, name="n_grouped", align_bytes=64)
         n_codes = keep.tile([P, UP_PASSES, TOKEN_TILES, P], U32, name="n_codes", align_bytes=64)
@@ -194,14 +195,13 @@ def tile_mhlattention_pa_kernel(tc, x, w_down, rms_w, w_up, out_0, out_1, out_2,
             step_blocks[s] = [block_of(BLOCKS * s + i) for i in range(BLOCKS)]
             two = grouped_pool.tile([P, 2 * BANK * PACK], BF16, name="two", tag="two", bufs=2, align_bytes=64)
             one = grouped_pool.tile([P, BANK * PACK], BF16, name="grouped", tag="grouped", align_bytes=64)
-            if 0 < s < DOWN_PASSES + UP_PASSES:
+            if 0 < s < DOWN_PASSES + UP_PASSES and s not in EXTRA:
                 both = raw_rows[s][:, :, 0 : 2 * BANK].rearrange("p t (c i) -> p t c i", i=4)
                 lay_out(nc.vector.tensor_copy, both, two[:])
             else:
                 for i in range(2):
-                    lay_out(
-                        nc.vector.tensor_copy, step_blocks[s][i][0], two[:, BANK * PACK * i : BANK * PACK * (i + 1)]
-                    )
+                    copy = nc.scalar.copy if i == 1 and s in EXTRA else nc.vector.tensor_copy
+                    lay_out(copy, step_blocks[s][i][0], two[:, BANK * PACK * i : BANK * PACK * (i + 1)])
             lay_out(nc.scalar.copy, step_blocks[s][2][0], one[:])
             step_grouped[s] = (two, one)
             if s < DOWN_PASSES + UP_PASSES:
@@ -352,7 +352,7 @@ def tile_mhlattention_pa_kernel(tc, x, w_down, rms_w, w_up, out_0, out_1, out_2,
         staged = {}
         split = 2 * HEADS * NOPE
 
-        qkv_banks = {}
+        unturned = {}
 
         def views(third, pair):
             whole_tile = staged[(third, pair)]
@@ -367,7 +367,10 @@ def tile_mhlattention_pa_kernel(tc, x, w_down, rms_w, w_up, out_0, out_1, out_2,
             tiles = [2 * pair + tl for pair in pairs for tl in range(2)]
             filled = {}
             for t in tiles:
-                filled[t] = sum_bank([P, BANK], "qkv_bank")
+                if t == TOKEN_TILES - 1:
+                    filled[t] = move_bank([P, BANK], F32, "qkv_bank")
+                else:
+                    filled[t] = sum_bank([P, BANK], "qkv_bank")
             for g in range(UP_PASSES):
                 for t in tiles:
                     nc.tensor.matmul_mx(
@@ -390,8 +393,13 @@ def tile_mhlattention_pa_kernel(tc, x, w_down, rms_w, w_up, out_0, out_1, out_2,
                     target = rope[:, :, tl, :]
                 else:
                     target = plain[:, HEAD_PAIRS[b], tl, :]
+                source = filled[t][:]
+                if third != V and b == 2:
+                    target = target[:, :, ROTATED:]
+                    source = source[:, HEADS * ROTATED :]
+                    unturned[(third, t)] = filled[t]
                 heads = target.shape[1]
-                copies[t % len(copies)](out=target, in_=filled[t][:].rearrange("p (d h) -> p h d", h=heads))
+                copies[t % len(copies)](out=target, in_=source.rearrange("p (d h) -> p h d", h=heads))
 
         def store_plain(third, pair, heads):
             tokens = slice(2 * pair, 2 * pair + 2)
@@ -400,35 +408,30 @@ def tile_mhlattention_pa_kernel(tc, x, w_down, rms_w, w_up, out_0, out_1, out_2,
                 in_=views(third, pair)[0][:, heads, :, :],
             )
 
-        def rotate(third, pair):
-            rope = views(third, pair)[1]
-            rope_out = outputs[third][1]
-            tokens = slice(2 * pair, 2 * pair + 2)
-            rotated = rope[:, :, :, 0:ROTATED]
-            partner = rotated.rearrange("p h t (i e) -> p h t i e", e=2)
-            swapped = swap_pool.tile([P, HEADS, 2, 2, PAIRS], F32, name="swapped", tag="swapped")
-            for e in range(2):
-                nc.vector.tensor_tensor(
-                    out=swapped[:, :, :, e, :],
-                    in0=partner[:, :, :, :, 1 - e],
-                    in1=sin_sign[:, tokens, e, :].unsqueeze(1).to_broadcast([P, HEADS, 2, PAIRS]),
-                    op=ALU.mult,
-                )
+        def rotate(third, t, bank):
+            pair, tl = divmod(t, 2)
+            r = bank[:, 0 : HEADS * ROTATED]
+            turned = views(third, pair)[1][:, :, tl, 0:ROTATED]
+            swapped = swap_pool.tile([P, HEADS, ROTATED], F32, name="swapped", tag="swapped")
             nc.vector.tensor_tensor(
-                out=rotated,
-                in0=rotated,
-                in1=cos_rep[:, tokens, :, :]
-                .rearrange("p t i e -> p t (i e)")
-                .unsqueeze(1)
-                .to_broadcast([P, HEADS, 2, ROTATED]),
+                out=swapped[:].rearrange("p h (i e) -> p h i e", e=2),
+                in0=r.rearrange("p (i e h) -> p h i e", e=2, h=HEADS)[:, :, :, ::-1],
+                in1=sin_sign[:, t, :, :].unsqueeze(1).to_broadcast([P, HEADS, PAIRS, 2]),
                 op=ALU.mult,
             )
-            rows = rotated.rearrange("p h t (i e) -> p (h t) i e", e=2)
             nc.vector.tensor_tensor(
-                out=rows, in0=rows, in1=swapped[:].rearrange("p h t e i -> p (h t) i e"), op=ALU.add
+                out=turned,
+                in0=r.rearrange("p (d h) -> p h d", h=HEADS),
+                in1=cos_rep[:, t, :, :].rearrange("p i e -> p (i e)").unsqueeze(1).to_broadcast([P, HEADS, ROTATED]),
+                op=ALU.mult,
             )
+            nc.vector.tensor_tensor(out=turned, in0=turned, in1=swapped[:], op=ALU.add)
+
+        def store_rope(third, pair):
+            tokens = slice(2 * pair, 2 * pair + 2)
             nc.sync.dma_start(
-                out=rope_out[0].rearrange("h (p t) d -> p h t d", t=TOKEN_TILES)[:, :, tokens, :], in_=rope
+                out=outputs[third][1][0].rearrange("h (p t) d -> p h t d", t=TOKEN_TILES)[:, :, tokens, :],
+                in_=views(third, pair)[1],
             )
 
         with tc.tile_pool(name="first", bufs=1) as first_pool:
@@ -444,9 +447,9 @@ def tile_mhlattention_pa_kernel(tc, x, w_down, rms_w, w_up, out_0, out_1, out_2,
             fetch_x(1)
             for load in range(2, DOWN_PASSES):
                 fetch_next()
-            nc.sync.dma_start(out=gain[:], in_=rms_w.partition_broadcast(P))
             for load in range(DOWN_PASSES, RAW_BUFS):
                 fetch_next()
+            nc.sync.dma_start(out=gain[:], in_=rms_w.partition_broadcast(P))
             angles()
             rope_tables()
             prepare(2, 0)
@@ -505,6 +508,8 @@ def tile_mhlattention_pa_kernel(tc, x, w_down, rms_w, w_up, out_0, out_1, out_2,
                     for pair in range(TOKEN_PAIRS):
                         store_plain(third, pair, HEAD_PAIRS[b])
                 prepare(s + 3, 1)
-                if part == 1:
-                    rotate(third, 0)
-                    rotate(third, 1)
+                if part == 0:
+                    for pair in range(TOKEN_PAIRS):
+                        for t in (2 * pair, 2 * pair + 1):
+                            rotate(third, t, unturned[(third, t)])
+                        store_rope(third, pair)

@@ -17,8 +17,7 @@ P = 128
 PACK = 4
 K_PASS = P * PACK
 BANK = 512
-SUM_BANKS = 6
-MOVE_BANKS = 2
+PSUM_BANKS = 8
 
 TOKENS = 512
 TOKEN_TILES = TOKENS // P
@@ -62,13 +61,10 @@ def tile_mhlattention_pa_kernel(tc, x, w_down, rms_w, w_up, out_0, out_1, out_2,
         up_pool = pools.enter_context(tc.tile_pool(name="up", bufs=5))
         keep = pools.enter_context(tc.tile_pool(name="keep", bufs=1))
         norm_pool = pools.enter_context(tc.tile_pool(name="norm", bufs=2))
-        psum = pools.enter_context(tc.psum_pool(name="psum", bufs=SUM_BANKS))
+        banks = pools.enter_context(tc.psum_pool(name="banks", bufs=PSUM_BANKS))
 
-        def sum_bank(shape, name):
-            return psum.tile(shape, F32, name=name, tag="sums", bufs=SUM_BANKS)
-
-        def move_bank(shape, dtype, name):
-            return psum.tile(shape, dtype, name=name, tag="moves", bufs=MOVE_BANKS)
+        def new_bank(shape, name):
+            return banks.tile(shape, F32, name=name, tag="bank")
 
         pos_int = consts.tile([P, TOKEN_TILES], I32, name="pos_int")
         nc.gpsimd.iota(pos_int[:], pattern=[[1, TOKEN_TILES]], base=0, channel_multiplier=TOKEN_TILES)
@@ -255,7 +251,7 @@ def tile_mhlattention_pa_kernel(tc, x, w_down, rms_w, w_up, out_0, out_1, out_2,
                 x_words = x_grouped[:].bitcast(F32).rearrange("q (g t u) -> q g t u", g=2, u=2)
                 for gg in range(2):
                     g = 2 * half + gg
-                    flipped = sum_bank([P, 2, 2 * P], "x_flipped")
+                    flipped = new_bank([P, 2, 2 * P], "x_flipped")
                     for u in range(2):
                         for tl in range(2):
                             nc.tensor.transpose(
@@ -273,24 +269,21 @@ def tile_mhlattention_pa_kernel(tc, x, w_down, rms_w, w_up, out_0, out_1, out_2,
 
         h_banks = {}
 
-        def open_h_banks(t):
-            for b in range(BLOCKS):
-                h_banks[(t, b)] = sum_bank([P, BANK], "h_bank")
-
-        def first_pass(t, g):
+        def first_pass(t, b, g):
+            if g == 0:
+                h_banks[(t, b)] = new_bank([P, BANK], "h_bank")
             pair, tl = divmod(t, 2)
             tok = slice(P * tl, P * (tl + 1))
-            for b in range(BLOCKS):
-                cols = slice(BANK * b, BANK * (b + 1))
-                nc.tensor.matmul_mx(
-                    out=h_banks[(t, b)][:],
-                    lhsT=x_codes[:, pair, g, tok].bitcast(FP8X4),
-                    lhsT_scale=x_scales[:, pair, g, tok],
-                    rhs=down_codes[:, g, cols].bitcast(FP8X4),
-                    rhs_scale=down_scales[:, g, cols],
-                    start=(g == 0),
-                    stop=(g == DOWN_PASSES - 1),
-                )
+            cols = slice(BANK * b, BANK * (b + 1))
+            nc.tensor.matmul_mx(
+                out=h_banks[(t, b)][:],
+                lhsT=x_codes[:, pair, g, tok].bitcast(FP8X4),
+                lhsT_scale=x_scales[:, pair, g, tok],
+                rhs=down_codes[:, g, cols].bitcast(FP8X4),
+                rhs_scale=down_scales[:, g, cols],
+                start=(g == 0),
+                stop=(g == DOWN_PASSES - 1),
+            )
 
         def squares(t):
             for b in range(BLOCKS):
@@ -323,7 +316,7 @@ def tile_mhlattention_pa_kernel(tc, x, w_down, rms_w, w_up, out_0, out_1, out_2,
 
         def flip(pair):
             for g in range(UP_PASSES):
-                flipped = move_bank([P, 2, 2 * P], F32, "n_flipped")
+                flipped = new_bank([P, 2, 2 * P], "n_flipped")
                 for u in range(2):
                     for tl in range(2):
                         nc.tensor.transpose(
@@ -367,10 +360,7 @@ def tile_mhlattention_pa_kernel(tc, x, w_down, rms_w, w_up, out_0, out_1, out_2,
             tiles = [2 * pair + tl for pair in pairs for tl in range(2)]
             filled = {}
             for t in tiles:
-                if t == TOKEN_TILES - 1:
-                    filled[t] = move_bank([P, BANK], F32, "qkv_bank")
-                else:
-                    filled[t] = sum_bank([P, BANK], "qkv_bank")
+                filled[t] = new_bank([P, BANK], "qkv_bank")
             for g in range(UP_PASSES):
                 for t in tiles:
                     nc.tensor.matmul_mx(
@@ -456,31 +446,32 @@ def tile_mhlattention_pa_kernel(tc, x, w_down, rms_w, w_up, out_0, out_1, out_2,
             quantise_x(0)
             quantise_x(1)
             for t in range(2):
-                open_h_banks(t)
-                for g in range(2):
-                    first_pass(t, g)
+                for b in range(BLOCKS):
+                    for g in range(2):
+                        first_pass(t, b, g)
             for g in range(2, DOWN_PASSES):
                 prepare(g + 1, 0)
                 for t in range(2):
-                    first_pass(t, g)
+                    for b in range(BLOCKS):
+                        first_pass(t, b, g)
             lay_to(5)
             squares(0)
             squares(1)
+            for b in range(2):
+                for g in range(DOWN_PASSES):
+                    first_pass(2, b, g)
             prepare(5, 1)
             scale(0)
             scale(1)
-            open_h_banks(2)
-            for g in range(2):
-                first_pass(2, g)
+            for g in range(DOWN_PASSES):
+                first_pass(2, 2, g)
             flip(0)
-            for g in range(2, 4):
-                first_pass(2, g)
             squares(2)
             prepare(6, 1)
             quantise_n(0)
-            open_h_banks(3)
-            for g in range(DOWN_PASSES):
-                first_pass(3, g)
+            for b in range(BLOCKS):
+                for g in range(DOWN_PASSES):
+                    first_pass(3, b, g)
             scale(2)
             squares(3)
             prepare(7, 1)

@@ -440,7 +440,9 @@ def tile_mhlattention_pa_kernel(tc, x, w_down, rms_w, w_up, out_0, out_1, out_2,
             for load in range(DOWN_PASSES, RAW_BUFS):
                 fetch_next()
             nc.sync.dma_start(out=gain[:], in_=rms_w.partition_broadcast(P))
-            angles()
+            with tc.manual_schedule():
+                angles()
+                lay_to(1)
             rope_tables()
             prepare(2, 0)
             quantise_x(0)

@@ -36,7 +36,7 @@ Q, K, V = 0, 1, 2
 TURN = (V, Q, K)
 COLUMN_TURN = (2, 0, 1)
 EPS = 1e-6
-EXTRA = (5,)
+EXTRA = (2, 5)
 HEAD_PAIRS = (slice(0, 2), slice(2, 4))
 
 DOWN_PASSES = D_MODEL // K_PASS

from contextlib import ExitStack

import concourse.mybir as mybir
from concourse.masks import make_identity

F32 = mybir.dt.float32
BF16 = mybir.dt.bfloat16
I32 = mybir.dt.int32
U32 = mybir.dt.uint32
U8 = mybir.dt.uint8
FP8X4 = mybir.dt.float8_e4m3fn_x4
ALU = mybir.AluOpType
ACT = mybir.ActivationFunctionType
AXIS = mybir.AxisListType

P = 128
PACK = 4
K_PASS = P * PACK
BANK = 512
PSUM_BANKS = 8

TOKENS = 512
TOKEN_TILES = TOKENS // P
TOKEN_PAIRS = TOKEN_TILES // 2
D_MODEL = 2048
LATENT = 1536
HEADS = 4
NOPE = 256
ROPE = 128
ROTATED = 64
PAIRS = ROTATED // 2
D_HEAD = NOPE + ROPE
THIRD = HEADS * D_HEAD
THIRDS = 3
Q, K, V = 0, 1, 2
TURN = (V, Q, K)
COLUMN_TURN = (2, 0, 1)
EPS = 1e-6
EXTRA = (2, 5)
HEAD_PAIRS = (slice(0, 2), slice(2, 4))

DOWN_PASSES = D_MODEL // K_PASS
UP_PASSES = LATENT // K_PASS
BLOCKS = LATENT // BANK
LOADS = DOWN_PASSES + THIRDS * UP_PASSES
STEPS = LOADS
GROUPED_BUFS = 3
RAW_BUFS = 6
TWO_PI = 6.283185307179586
ROUND_MAGIC = 12582912.0

FLOPS = 2 * TOKENS * (D_MODEL * LATENT + LATENT * THIRDS * THIRD)


def tile_mhlattention_pa_kernel(tc, x, w_down, rms_w, w_up, out_0, out_1, out_2, out_3, out_4):
    nc = tc.nc
    with ExitStack() as pools:
        consts = pools.enter_context(tc.tile_pool(name="consts", bufs=1))
        raw_pool = pools.enter_context(tc.tile_pool(name="raw", bufs=RAW_BUFS))
        grouped_pool = pools.enter_context(tc.tile_pool(name="grouped", bufs=GROUPED_BUFS))
        up_pool = pools.enter_context(tc.tile_pool(name="up", bufs=5))
        keep = pools.enter_context(tc.tile_pool(name="keep", bufs=1))
        norm_pool = pools.enter_context(tc.tile_pool(name="norm", bufs=2))
        banks = pools.enter_context(tc.psum_pool(name="banks", bufs=PSUM_BANKS))

        def new_bank(shape, name):
            return banks.tile(shape, F32, name=name, tag="bank")

        pos_int = consts.tile([P, TOKEN_TILES], I32, name="pos_int")
        nc.gpsimd.iota(pos_int[:], pattern=[[1, TOKEN_TILES]], base=0, channel_multiplier=TOKEN_TILES)
        ident_f32 = consts.tile([P, P], F32, name="ident_f32")
        make_identity(nc, ident_f32[:])
        gain = consts.tile([P, LATENT], BF16, name="gain")

        pos = consts.tile([P, TOKEN_TILES], F32, name="pos")
        turns = consts.tile([P, 2, PAIRS, TOKEN_TILES], F32, name="turns")
        whole = consts.tile([P, 2, PAIRS, TOKEN_TILES], F32, name="whole")
        frac = consts.tile([P, 2, PAIRS, TOKEN_TILES], F32, name="frac")
        trig = consts.tile([P, 2, PAIRS, TOKEN_TILES], F32, name="trig")
        cos_rep = consts.tile([P, TOKEN_TILES, PAIRS, 2], F32, name="cos_rep")
        sin_sign = consts.tile([P, TOKEN_TILES, PAIRS, 2], F32, name="sin_sign")
        one = consts.tile([P, 1], F32, name="one")
        one_root = consts.tile([P, 1], F32, name="one_root")

        def angles():
            nc.vector.memset(one[:], 1.0)
            nc.scalar.activation(out=one_root[:], in_=one[:], func=ACT.Sin)
            nc.vector.tensor_copy(out=pos[:], in_=pos_int[:])
            nc.vector.tensor_scalar_mul(out=turns[:, 0, 0, :], in0=pos[:], scalar1=1.0 / TWO_PI)
            ready = 1
            while ready < PAIRS:
                nc.vector.tensor_scalar_mul(
                    out=turns[:, 0, ready : 2 * ready, :],
                    in0=turns[:, 0, 0:ready, :],
                    scalar1=10000.0 ** (-ready / PAIRS),
                )
                ready *= 2
            nc.vector.tensor_scalar_add(out=turns[:, 1, :, :], in0=turns[:, 0, :, :], scalar1=0.25)
            nc.vector.tensor_scalar(
                out=whole[:], in0=turns[:], scalar1=ROUND_MAGIC, scalar2=ROUND_MAGIC, op0=ALU.add, op1=ALU.subtract
            )
            nc.vector.tensor_tensor(out=frac[:], in0=turns[:], in1=whole[:], op=ALU.subtract)
            nc.scalar.activation(out=trig[:], in_=frac[:], func=ACT.Sin, scale=TWO_PI)
            nc.scalar.activation(out=one_root[:], in_=one[:], func=ACT.Sqrt)

        def rope_tables():
            nc.vector.tensor_copy(
                out=cos_rep[:],
                in_=trig[:, 1, :, :]
                .rearrange("p i t -> p t i")
                .unsqueeze(3)
                .to_broadcast([P, TOKEN_TILES, PAIRS, 2]),
            )
            nc.vector.tensor_scalar_mul(
                out=sin_sign[:, :, :, 0], in0=trig[:, 0, :, :].rearrange("p i t -> p t i"), scalar1=-1.0
            )
            nc.vector.tensor_copy(out=sin_sign[:, :, :, 1], in_=trig[:, 0, :, :].rearrange("p i t -> p t i"))

        n_grouped = keep.tile([P, UP_PASSES, TOKEN_TILES, P * PACK], BF16, name="n_grouped", align_bytes=64)
        n_codes = keep.tile([P, UP_PASSES, TOKEN_TILES, P], U32, name="n_codes", align_bytes=64)
        n_scales = keep.tile([P, UP_PASSES, TOKEN_TILES, P], U8, name="n_scales", align_bytes=64)
        sum_sq = keep.tile([P, TOKEN_TILES, BLOCKS], F32, name="sum_sq")
        sum_copy = keep.tile([P, TOKEN_TILES, BLOCKS], F32, name="sum_copy")
        total_sq = keep.tile([P, TOKEN_TILES], F32, name="total_sq")
        rms = keep.tile([P, TOKEN_TILES], F32, name="rms")
        rstd = keep.tile([P, TOKEN_TILES], F32, name="rstd")


        raw_rows = {}
        step_blocks = {}
        step_grouped = {}
        up_codes = {}
        up_scales = {}
        asked = [0]

        def fetch_next():
            load = asked[0]
            asked[0] += 1
            if load >= LOADS:
                return
            if load == 0:
                raw = raw_pool.tile([P, BLOCKS, PACK, BANK], BF16, name="raw", tag="raw")
                for i in range(BLOCKS):
                    rows = w_down[0:K_PASS, BANK * i : BANK * (i + 1)]
                    nc.sync.dma_start(out=raw[:, i, :, :], in_=rows.rearrange("(p t) c -> p t c", t=PACK))
                raw_rows[load] = raw
                return
            raw = raw_pool.tile([P, PACK, LATENT], BF16, name="raw", tag="raw")
            raw_rows[load] = raw
            if load < DOWN_PASSES:
                rows = w_down[K_PASS * load : K_PASS * (load + 1), :]
                nc.sync.dma_start(out=raw[:], in_=rows.rearrange("(p t) c -> p t c", t=PACK))
            else:
                place, g = divmod(load - DOWN_PASSES, UP_PASSES)
                third = TURN[place]
                rows = w_up[K_PASS * g : K_PASS * (g + 1), THIRD * third : THIRD * (third + 1)]
                nc.sync.dma_start(out=raw[:], in_=rows.rearrange("(p t) c -> p t c", t=PACK))

        def block_of(k):
            s, i = divmod(k, BLOCKS)
            if s < DOWN_PASSES:
                cols = slice(BANK * i, BANK * (i + 1))
                raw = raw_rows[s][:, i, :, :] if s == 0 else raw_rows[s][:, :, cols]
                raw = raw.rearrange("p t (c i) -> p t c i", i=4)
                return raw, down_codes[:, s, cols], down_scales[:, s, cols]
            place, part = divmod(s - DOWN_PASSES, BLOCKS)
            third = TURN[place]
            g, b = (part, i) if place == 0 else (i, COLUMN_TURN[part])
            if (third, b) not in up_codes:
                up_codes[(third, b)] = up_pool.tile(
                    [P, UP_PASSES * BANK], U32, name="up_codes", tag="up_codes", align_bytes=64
                )
                up_scales[(third, b)] = up_pool.tile(
                    [P, UP_PASSES * BANK], U8, name="up_scales", tag="up_scales", align_bytes=64
                )
            raw = raw_rows[DOWN_PASSES + UP_PASSES * place + g]
            if third != V and b < 2:
                raw = raw[:, :, 0 : HEADS * NOPE].rearrange("p t (d h) -> p t d h", h=HEADS)[:, :, :, HEAD_PAIRS[b]]
            else:
                raw = raw[:, :, BANK * b : BANK * (b + 1)].rearrange("p t (d h) -> p t d h", h=HEADS)
            words = slice(BANK * g, BANK * (g + 1))
            return raw, up_codes[(third, b)][:, words], up_scales[(third, b)][:, words]

        def lay_out(copy, raw, grouped):
            copy(
                out=grouped.rearrange("p (c i t) -> p c t i", i=raw.shape[3], t=PACK),
                in_=raw.rearrange("p t c i -> p c t i"),
            )

        def lay(s):
            step_blocks[s] = [block_of(BLOCKS * s + i) for i in range(BLOCKS)]
            two = grouped_pool.tile([P, 2 * BANK * PACK], BF16, name="two", tag="two", bufs=2, align_bytes=64)
            one = grouped_pool.tile([P, BANK * PACK], BF16, name="grouped", tag="grouped", align_bytes=64)
            if 0 < s < DOWN_PASSES + UP_PASSES and s not in EXTRA:
                both = raw_rows[s][:, :, 0 : 2 * BANK].rearrange("p t (c i) -> p t c i", i=4)
                lay_out(nc.vector.tensor_copy, both, two[:])
            else:
                for i in range(2):
                    copy = nc.scalar.copy if i == 1 and s in EXTRA else nc.vector.tensor_copy
                    lay_out(copy, step_blocks[s][i][0], two[:, BANK * PACK * i : BANK * PACK * (i + 1)])
            lay_out(nc.scalar.copy, step_blocks[s][2][0], one[:])
            step_grouped[s] = (two, one)
            if s < DOWN_PASSES + UP_PASSES:
                fetch_next()

        def quantise_two(s):
            two = step_grouped[s][0]
            if s < DOWN_PASSES:
                quantize(two[:], down_codes[:, s, 0 : 2 * BANK], down_scales[:, s, 0 : 2 * BANK])
            elif s < DOWN_PASSES + UP_PASSES:
                for i in range(2):
                    quantize(two[:, BANK * PACK * i : BANK * PACK * (i + 1)], step_blocks[s][i][1], step_blocks[s][i][2])
            else:
                place, part = divmod(s - DOWN_PASSES, BLOCKS)
                block = (TURN[place], COLUMN_TURN[part])
                quantize(two[:], up_codes[block][:, 0 : 2 * BANK], up_scales[block][:, 0 : 2 * BANK])

        def quantise_one(s):
            quantize(step_grouped[s][1][:], step_blocks[s][2][1], step_blocks[s][2][2])

        def quantize(grouped, codes, scales):
            nc.vector.quantize_mx(out=codes.bitcast(FP8X4), scales=scales, in_=grouped)

        done = {"laid": 0, "quantised": 0}

        def lay_to(s):
            while done["laid"] < min(s, STEPS):
                lay(done["laid"])
                done["laid"] += 1

        def prepare(s, lead):
            while done["quantised"] < min(s, STEPS):
                lay_to(done["quantised"] + 1)
                quantise_two(done["quantised"])
                lay_to(done["quantised"] + 1 + lead)
                quantise_one(done["quantised"])
                done["quantised"] += 1

        x_raw = {}

        def fetch_x(pair):
            x_raw[pair] = first_pool.tile([P, 2, D_MODEL], BF16, name="x_raw", tag="x_raw", bufs=TOKEN_PAIRS)
            nc.sync.dma_start(
                out=x_raw[pair][:],
                in_=x[0].rearrange("(p t) k -> p t k", t=TOKEN_TILES)[:, 2 * pair : 2 * pair + 2, :],
            )

        def quantise_x(pair):
            for half in range(DOWN_PASSES // 2):
                x_grouped = grouped_pool.tile([P, BANK * PACK], BF16, name="x_grouped", tag="grouped", align_bytes=64)
                x_words = x_grouped[:].bitcast(F32).rearrange("q (g t u) -> q g t u", g=2, u=2)
                for gg in range(2):
                    g = 2 * half + gg
                    flipped = new_bank([P, 2, 2 * P], "x_flipped")
                    for u in range(2):
                        for tl in range(2):
                            nc.tensor.transpose(
                                flipped[:, u, P * tl : P * (tl + 1)],
                                x_raw[pair][:, tl, :].bitcast(F32)[:, 256 * g + u : 256 * (g + 1) : 2],
                                ident_f32[:],
                            )
                    nc.scalar.copy(out=x_words[:, gg, :, :], in_=flipped[:].rearrange("q u t -> q t u"))
                passes = slice(2 * half, 2 * half + 2)
                nc.vector.quantize_mx(
                    out=x_codes[:, pair, passes, :].rearrange("q g t -> q (g t)").bitcast(FP8X4),
                    scales=x_scales[:, pair, passes, :].rearrange("q g t -> q (g t)"),
                    in_=x_grouped[:],
                )

        h_banks = {}

        def first_pass(t, b, g):
            if g == 0:
                h_banks[(t, b)] = new_bank([P, BANK], "h_bank")
            pair, tl = divmod(t, 2)
            tok = slice(P * tl, P * (tl + 1))
            cols = slice(BANK * b, BANK * (b + 1))
            nc.tensor.matmul_mx(
                out=h_banks[(t, b)][:],
                lhsT=x_codes[:, pair, g, tok].bitcast(FP8X4),
                lhsT_scale=x_scales[:, pair, g, tok],
                rhs=down_codes[:, g, cols].bitcast(FP8X4),
                rhs_scale=down_scales[:, g, cols],
                start=(g == 0),
                stop=(g == DOWN_PASSES - 1),
            )

        def squares(t):
            for b in range(BLOCKS):
                unread = norm_pool.tile([P, BANK], BF16, name="unread", tag="unread", bufs=2)
                nc.scalar.activation(
                    out=unread[:], in_=h_banks[(t, b)][:], func=ACT.Square, accum_out=sum_sq[:, t, b : b + 1]
                )
            nc.scalar.activation(
                out=sum_copy[:, t, :], in_=sum_sq[:, t, :], func=ACT.Copy, accum_out=total_sq[:, t : t + 1]
            )
            nc.scalar.activation(
                out=rms[:, t : t + 1], in_=total_sq[:, t : t + 1], func=ACT.Sqrt, scale=1.0 / LATENT, bias=EPS
            )

        n_bf = {}

        def scale(t):
            nc.vector.reciprocal(out=rstd[:, t : t + 1], in_=rms[:, t : t + 1])
            n_bf[t] = norm_pool.tile([P, LATENT], BF16, name="n_bf", tag="n_bf", bufs=4)
            for b in range(BLOCKS):
                cols = slice(BANK * b, BANK * (b + 1))
                nc.vector.scalar_tensor_tensor(
                    out=n_bf[t][:, cols],
                    in0=h_banks[(t, b)][:],
                    scalar=rstd[:, t : t + 1],
                    in1=gain[:, cols],
                    op0=ALU.mult,
                    op1=ALU.mult,
                )

        def flip(pair):
            for g in range(UP_PASSES):
                flipped = new_bank([P, 2, 2 * P], "n_flipped")
                for u in range(2):
                    for tl in range(2):
                        nc.tensor.transpose(
                            flipped[:, u, P * tl : P * (tl + 1)],
                            n_bf[2 * pair + tl][:].bitcast(F32)[:, 256 * g + u : 256 * (g + 1) : 2],
                            ident_f32[:],
                        )
                nc.scalar.copy(
                    out=n_grouped[:, g, 2 * pair : 2 * pair + 2, :]
                    .rearrange("p t c -> p (t c)")
                    .bitcast(F32)
                    .rearrange("q (r u) -> q r u", u=2),
                    in_=flipped[:].rearrange("q u r -> q r u"),
                )

        def quantise_n(pair):
            two = slice(2 * pair, 2 * pair + 2)
            for g in range(UP_PASSES):
                nc.vector.quantize_mx(
                    out=n_codes[:, g, two, :].rearrange("p t r -> p (t r)").bitcast(FP8X4),
                    scales=n_scales[:, g, two, :].rearrange("p t r -> p (t r)"),
                    in_=n_grouped[:, g, two, :].rearrange("p t c -> p (t c)"),
                )

        outputs = [(out_0, out_1), (out_2, out_3), (out_4, None)]
        staged = {}
        split = 2 * HEADS * NOPE

        unturned = {}

        def views(third, pair):
            whole_tile = staged[(third, pair)]
            if outputs[third][1] is None:
                return whole_tile[:].rearrange("p (h t d) -> p h t d", h=HEADS, t=2), None
            return (
                whole_tile[:, 0:split].rearrange("p (h t d) -> p h t d", h=HEADS, t=2),
                whole_tile[:, split:].rearrange("p (h t d) -> p h t d", h=HEADS, t=2),
            )

        def second(third, b, pairs, copies):
            tiles = [2 * pair + tl for pair in pairs for tl in range(2)]
            filled = {}
            for t in tiles:
                filled[t] = new_bank([P, BANK], "qkv_bank")
            for g in range(UP_PASSES):
                for t in tiles:
                    nc.tensor.matmul_mx(
                        out=filled[t][:],
                        lhsT=n_codes[:, g, t, :].bitcast(FP8X4),
                        lhsT_scale=n_scales[:, g, t, :],
                        rhs=up_codes[(third, b)][:, BANK * g : BANK * (g + 1)].bitcast(FP8X4),
                        rhs_scale=up_scales[(third, b)][:, BANK * g : BANK * (g + 1)],
                        start=(g == 0),
                        stop=(g == UP_PASSES - 1),
                    )
            for t in tiles:
                pair, tl = divmod(t, 2)
                if (third, pair) not in staged:
                    staged[(third, pair)] = stage_pool.tile([P, 2 * THIRD], F32, name="staged", tag="staged")
                plain, rope = views(third, pair)
                if third == V:
                    target = plain[:, :, tl, P * b : P * (b + 1)]
                elif b == 2:
                    target = rope[:, :, tl, :]
                else:
                    target = plain[:, HEAD_PAIRS[b], tl, :]
                source = filled[t][:]
                if third != V and b == 2:
                    target = target[:, :, ROTATED:]
                    source = source[:, HEADS * ROTATED :]
                    unturned[(third, t)] = filled[t]
                heads = target.shape[1]
                copies[t % len(copies)](out=target, in_=source.rearrange("p (d h) -> p h d", h=heads))

        def store_plain(third, pair, heads):
            tokens = slice(2 * pair, 2 * pair + 2)
            nc.sync.dma_start(
                out=outputs[third][0][0].rearrange("h (p t) d -> p h t d", t=TOKEN_TILES)[:, heads, tokens, :],
                in_=views(third, pair)[0][:, heads, :, :],
            )

        def rotate(third, t, bank):
            pair, tl = divmod(t, 2)
            r = bank[:, 0 : HEADS * ROTATED]
            turned = views(third, pair)[1][:, :, tl, 0:ROTATED]
            swapped = swap_pool.tile([P, HEADS, ROTATED], F32, name="swapped", tag="swapped")
            nc.vector.tensor_tensor(
                out=swapped[:].rearrange("p h (i e) -> p h i e", e=2),
                in0=r.rearrange("p (i e h) -> p h i e", e=2, h=HEADS)[:, :, :, ::-1],
                in1=sin_sign[:, t, :, :].unsqueeze(1).to_broadcast([P, HEADS, PAIRS, 2]),
                op=ALU.mult,
            )
            nc.vector.tensor_tensor(
                out=turned,
                in0=r.rearrange("p (d h) -> p h d", h=HEADS),
                in1=cos_rep[:, t, :, :].rearrange("p i e -> p (i e)").unsqueeze(1).to_broadcast([P, HEADS, ROTATED]),
                op=ALU.mult,
            )
            nc.vector.tensor_tensor(out=turned, in0=turned, in1=swapped[:], op=ALU.add)

        def store_rope(third, pair):
            tokens = slice(2 * pair, 2 * pair + 2)
            nc.sync.dma_start(
                out=outputs[third][1][0].rearrange("h (p t) d -> p h t d", t=TOKEN_TILES)[:, :, tokens, :],
                in_=views(third, pair)[1],
            )

        with tc.tile_pool(name="first", bufs=1) as first_pool:
            down_codes = first_pool.tile([P, DOWN_PASSES, LATENT], U32, name="down_codes", align_bytes=64)
            down_scales = first_pool.tile([P, DOWN_PASSES, LATENT], U8, name="down_scales", align_bytes=64)
            x_codes = first_pool.tile([P, TOKEN_PAIRS, DOWN_PASSES, 2 * P], U32, name="x_codes", align_bytes=64)
            x_scales = first_pool.tile([P, TOKEN_PAIRS, DOWN_PASSES, 2 * P], U8, name="x_scales", align_bytes=64)
            by_scalar = [nc.scalar.copy]
            by_both = [nc.scalar.copy, nc.vector.tensor_copy]
            for load in range(2):
                fetch_next()
            fetch_x(0)
            fetch_x(1)
            for load in range(2, DOWN_PASSES):
                fetch_next()
            for load in range(DOWN_PASSES, RAW_BUFS):
                fetch_next()
            nc.sync.dma_start(out=gain[:], in_=rms_w.partition_broadcast(P))
            with tc.manual_schedule():
                angles()
                lay_to(1)
            rope_tables()
            prepare(2, 0)
            quantise_x(0)
            quantise_x(1)
            for t in range(2):
                for b in range(BLOCKS):
                    for g in range(2):
                        first_pass(t, b, g)
            for g in range(2, DOWN_PASSES):
                prepare(g + 1, 0)
                for t in range(2):
                    for b in range(BLOCKS):
                        first_pass(t, b, g)
            lay_to(5)
            squares(0)
            squares(1)
            for b in range(2):
                for g in range(DOWN_PASSES):
                    first_pass(2, b, g)
            prepare(5, 1)
            scale(0)
            scale(1)
            for g in range(DOWN_PASSES):
                first_pass(2, 2, g)
            flip(0)
            squares(2)
            prepare(6, 1)
            quantise_n(0)
            for b in range(BLOCKS):
                for g in range(DOWN_PASSES):
                    first_pass(3, b, g)
            scale(2)
            squares(3)
            prepare(7, 1)
        with tc.tile_pool(name="stage", bufs=4, reuse_waits="tile") as stage_pool, tc.tile_pool(
            name="swap", bufs=2, reuse_waits="tile"
        ) as swap_pool:
            scale(3)
            second(V, 0, [0], by_scalar)
            flip(1)
            quantise_n(1)
            prepare(8, 1)
            second(V, 1, [0], by_scalar)
            second(V, 2, [0], by_scalar)
            store_plain(V, 0, slice(0, HEADS))
            for b in range(BLOCKS):
                second(V, b, [1], by_scalar)
            store_plain(V, 1, slice(0, HEADS))
            prepare(9, 1)
            for s in range(DOWN_PASSES + BLOCKS, STEPS):
                place, part = divmod(s - DOWN_PASSES, BLOCKS)
                third = TURN[place]
                b = COLUMN_TURN[part]
                second(third, b, [0, 1], by_both if s + 1 == STEPS else by_scalar)
                if b < 2:
                    for pair in range(TOKEN_PAIRS):
                        store_plain(third, pair, HEAD_PAIRS[b])
                prepare(s + 3, 1)
                if part == 0:
                    for pair in range(TOKEN_PAIRS):
                        for t in (2 * pair, 2 * pair + 1):
                            rotate(third, t, unturned[(third, t)])
                        store_rope(third, pair)
